import numpy as np
import ml_dtypes


def mxq(x, axis, fmt="e4m3"):
    dtype, down = {"e4m3": (ml_dtypes.float8_e4m3fn, 7), "e5m2": (ml_dtypes.float8_e5m2, 14)}[fmt]
    v = np.moveaxis(np.asarray(x, np.float32).astype(ml_dtypes.bfloat16).astype(np.float64), axis, -1)
    blocks = v.reshape(v.shape[:-1] + (-1, 32))
    amax = np.abs(blocks).max(-1, keepdims=True)
    byte = np.maximum(np.where(amax > 0, np.frexp(amax)[1] - 1 + 127, 0) - down, 1)
    scale = np.exp2(byte - 127.0)
    codes = (blocks / scale).astype(np.float32).astype(dtype).astype(np.float64)
    return np.moveaxis((codes * scale).reshape(v.shape), -1, axis)


WIDE = False


def mx_kscale(k):
    if not WIDE:
        return np.ones(k)
    levels = np.array([10, -10, 5, -5, 0])
    a = np.random.permutation(np.resize(levels, k // 512 * 4)).reshape(k // 512, 4)
    idx = np.arange(k)
    return np.exp2(a[idx // 512, idx % 128 // 32])


BF16 = ml_dtypes.bfloat16


def bf(x):
    return np.asarray(x, np.float32).astype(BF16)


def f64(x):
    return np.asarray(x).astype(np.float64)


N, C, T, V, H, O = 4, 512, 64, 25, 512, 256


def setup_inputs():
    s = mx_kscale(C)
    wscale = 0.7 * np.sqrt(V / C)
    return {
        "xm": bf(np.random.standard_normal((N, C, T)) / np.sqrt(V) * s[None, :, None]),
        "Wq": bf(np.random.standard_normal((H, C)) * wscale / s[None, :]),
        "bq": bf(np.random.standard_normal(H) * 0.3),
        "Wk": bf(np.random.standard_normal((H, C)) * wscale / s[None, :]),
        "bk": bf(np.random.standard_normal(H) * 0.3),
        "Wr": bf(np.random.standard_normal((O, H)) / np.sqrt(H)),
        "br": bf(np.random.standard_normal(O) * 0.3),
    }


def reference(xm, Wq, bq, Wk, bk, Wr, br):
    xq = mxq(f64(xm), 1, "e4m3")
    q = (mxq(f64(Wq), 1, "e4m3") @ xq) + f64(bq)[None, :, None]
    k = (mxq(f64(Wk), 1, "e4m3") @ xq) + f64(bk)[None, :, None]
    d = np.tanh(q[:, :, :, None] - k[:, :, None, :])
    m = mxq(f64(Wr), 1, "e4m3") @ mxq(d, 1, "e4m3").reshape(N, H, T * T)
    return m.reshape(N, O, T, T) + f64(br)[None, :, None, None]

@@ -1,0 +1,199 @@
+import concourse.mybir as mybir
+from concourse.masks import make_identity
+
+F32 = mybir.dt.float32
+BF16 = mybir.dt.bfloat16
+U32 = mybir.dt.uint32
+U8 = mybir.dt.uint8
+FP8X4 = mybir.dt.float8_e4m3fn_x4
+TANH = mybir.ActivationFunctionType.Tanh
+IDENTITY = mybir.ActivationFunctionType.Identity
+ADD = mybir.AluOpType.add
+
+SAMPLES, C, T, H, O = 4, 512, 64, 512, 256
+P = 128
+PACK = 4
+K = P * PACK
+O_TILES = O // P
+FRAMES = SAMPLES * T
+G_CHUNK = 8
+CHUNK = G_CHUNK * T
+CHUNKS_PER_SAMPLE = T // G_CHUNK
+
+FLOPS = 2 * 2 * H * C * FRAMES + 2 * O * H * SAMPLES * T * T
+
+
+def load_weight(nc, pool, weight, rows_per_partition, name):
+    rows = pool.tile([P, rows_per_partition * K], BF16, name=name)
+    source = weight.rearrange("(r a) k -> r (a k)", a=rows_per_partition)
+    for first in range(0, rows_per_partition * K, 2 * K):
+        nc.sync.dma_start(out=rows[:, first : first + 2 * K], in_=source[:, first : first + 2 * K])
+    return rows
+
+
+def transpose_weight(nc, pool, psum, identity, rows, rows_per_partition, name):
+    words = rows[:].bitcast(F32).rearrange("r (a p s) -> r a s p", a=rows_per_partition, s=2)
+    grouped = pool.tile([P, rows_per_partition * P * PACK], BF16, name=name, align_bytes=64)
+    grouped_words = grouped[:].bitcast(F32).rearrange("p (a r s) -> p a r s", a=rows_per_partition, s=2)
+    for pair in range(rows_per_partition // 2):
+        bank = psum.tile([P, 2, 2, P], F32, name="transposed")
+        for a in range(2):
+            for s in range(2):
+                nc.tensor.transpose(bank[:, a, s, :], words[:, 2 * pair + a, s, :], identity[:])
+        copy = nc.vector.tensor_copy if pair % 2 == 0 else nc.scalar.copy
+        copy(out=grouped_words[:, 2 * pair : 2 * pair + 2], in_=bank[:].rearrange("p a s r -> p a r s"))
+    return grouped
+
+
+def quantise(nc, pool, grouped, name):
+    columns = grouped.shape[1] // PACK
+    codes = pool.tile([P, columns], U32, name=name + "_codes", align_bytes=64)
+    scales = pool.tile([P, columns], U8, name=name + "_scales", align_bytes=64)
+    nc.vector.quantize_mx(out=codes[:].bitcast(FP8X4), scales=scales[:], in_=grouped)
+    return codes, scales
+
+
+def load_bias(nc, pool, bias, per_partition, name):
+    raw = pool.tile([P, per_partition], BF16, name=name)
+    nc.scalar.dma_start(out=raw[:], in_=bias.rearrange("(p a) -> p a", a=per_partition))
+    return raw
+
+
+def widen(nc, pool, raw, name):
+    wide = pool.tile([P, raw.shape[1]], F32, name=name)
+    nc.vector.tensor_copy(out=wide[:], in_=raw[:])
+    return wide
+
+
+def tile_ta_block_pa_t_kernel(tc, xm, Wq, bq, Wk, bk, Wr, br, out):
+    nc = tc.nc
+
+    def one_pass(acc, weight, columns, moving):
+        nc.tensor.matmul_mx(
+            out=acc,
+            lhsT=weight[0][:, columns].bitcast(FP8X4),
+            lhsT_scale=weight[1][:, columns],
+            rhs=moving[0][:].bitcast(FP8X4),
+            rhs_scale=moving[1][:],
+            start=True,
+            stop=True,
+        )
+
+    with tc.tile_pool(name="keep", bufs=1) as keep, tc.tile_pool(name="work", bufs=3) as work, tc.manual_schedule():
+        with tc.psum_pool(name="head_psum", bufs=4) as head_psum:
+            bq_raw = load_bias(nc, keep, bq, PACK, "bq_raw")
+            bk_raw = load_bias(nc, keep, bk, PACK, "bk_raw")
+            br_raw = load_bias(nc, keep, br, O_TILES, "br_raw")
+
+            zero = keep.tile([P, 1], F32)
+            nc.vector.memset(zero[:], 0.0)
+            unused = keep.tile([P, 1], F32)
+            nc.scalar.activation(out=unused[:], in_=zero[:], func=TANH)
+
+            identity = keep.tile([P, P], F32)
+            make_identity(nc, identity[:])
+
+            x_rows = keep.tile([P, SAMPLES, PACK, T], BF16)
+            nc.sync.dma_start(
+                out=x_rows[:].rearrange("p n i t -> p n (i t)"),
+                in_=xm.rearrange("n (p i) t -> p n (i t)", i=PACK),
+            )
+            wq_rows = load_weight(nc, keep, Wq, PACK, "wq_rows")
+            wk_rows = load_weight(nc, keep, Wk, PACK, "wk_rows")
+            wr_rows = load_weight(nc, keep, Wr, O_TILES, "wr_rows")
+
+            x_grouped = keep.tile([P, SAMPLES, T, PACK], BF16, align_bytes=64)
+            nc.vector.tensor_copy(out=x_grouped[:], in_=x_rows[:].rearrange("p n i t -> p n t i"))
+            x_mx = quantise(nc, keep, x_grouped[:].rearrange("p n t i -> p (n t i)"), "x")
+
+            wq_grouped = transpose_weight(nc, keep, head_psum, identity, wq_rows, PACK, "wq_grouped")
+            wk_grouped = transpose_weight(nc, keep, head_psum, identity, wk_rows, PACK, "wk_grouped")
+            wq_mx = quantise(nc, keep, wq_grouped[:], "wq")
+            wk_mx = quantise(nc, keep, wk_grouped[:], "wk")
+            wr_grouped = transpose_weight(nc, keep, head_psum, identity, wr_rows, O_TILES, "wr_grouped")
+            bq_wide = widen(nc, keep, bq_raw, "bq_wide")
+            bk_wide = widen(nc, keep, bk_raw, "bk_wide")
+            br_wide = widen(nc, keep, br_raw, "br_wide")
+
+            q_wide = keep.tile([P, PACK, FRAMES], F32)
+            k_wide = keep.tile([P, PACK, FRAMES], F32)
+            for j in range(PACK):
+                heads = slice(j * P, (j + 1) * P)
+                q_acc = head_psum.tile([P, FRAMES], F32, name="q_acc", bufs=2)
+                one_pass(q_acc[:], wq_mx, heads, x_mx)
+                nc.vector.tensor_scalar(
+                    out=q_wide[:, j, :], in0=q_acc[:], scalar1=bq_wide[:, j : j + 1], scalar2=None, op0=ADD
+                )
+                k_acc = head_psum.tile([P, FRAMES], F32, name="k_acc", bufs=2)
+                one_pass(k_acc[:], wk_mx, heads, x_mx)
+                nc.scalar.activation(
+                    out=k_wide[:, j, :], in_=k_acc[:], func=IDENTITY, bias=bk_wide[:, j : j + 1], scale=1.0
+                )
+            wr_mx = quantise(nc, keep, wr_grouped[:], "wr")
+
+        with tc.psum_pool(name="psum", bufs=4) as psum:
+
+            def differences(n, g_first):
+                planes = work.tile([P, PACK, G_CHUNK, T], BF16, name="planes")
+                for j in range(PACK):
+                    for g in range(G_CHUNK):
+                        frame = n * T + g_first + g
+                        nc.scalar.activation(
+                            out=planes[:, j, g, :],
+                            in_=k_wide[:, j, n * T : (n + 1) * T],
+                            func=TANH,
+                            bias=q_wide[:, j, frame : frame + 1],
+                            scale=-1.0,
+                        )
+                return planes
+
+            def regroup(planes):
+                grouped = work.tile([P, CHUNK, PACK], BF16, name="grouped", align_bytes=64)
+                nc.vector.tensor_copy(
+                    out=grouped[:].rearrange("p (c i) j -> p c j i", i=4),
+                    in_=planes[:].rearrange("p j g t -> p j (g t)").rearrange("p j (c i) -> p c j i", i=4),
+                )
+                return grouped
+
+            def mix(d_mx):
+                banks = []
+                for a in range(O_TILES):
+                    acc = psum.tile([P, CHUNK], F32, name="acc")
+                    one_pass(acc[:], wr_mx, slice(a * P, (a + 1) * P), d_mx)
+                    banks.append(acc)
+                return banks
+
+            def store(result, n, g_first):
+                columns = slice(g_first * T, (g_first + G_CHUNK) * T)
+                nc.sync.dma_start(
+                    out=out[n].rearrange("(p a) g t -> p a (g t)", a=O_TILES)[:, :, columns], in_=result[:]
+                )
+
+            chunks = [(n, g_first) for n in range(SAMPLES) for g_first in range(0, T, G_CHUNK)]
+            before = None
+            for n, g_first in chunks:
+                planes = differences(n, g_first)
+                grouped = regroup(planes)
+                if before is not None:
+                    banks, where = before
+                    result = work.tile([P, O_TILES, CHUNK], F32, name="result")
+                    nc.vector.tensor_scalar(
+                        out=result[:, 0, :], in0=banks[0][:], scalar1=br_wide[:, 0:1], scalar2=None, op0=ADD
+                    )
+                d_mx = quantise(nc, work, grouped[:].rearrange("p w j -> p (w j)"), "d")
+                if before is not None:
+                    nc.vector.tensor_scalar(
+                        out=result[:, 1, :], in0=banks[1][:], scalar1=br_wide[:, 1:2], scalar2=None, op0=ADD
+                    )
+                    store(result, where[0], where[1])
+                before = (mix(d_mx), (n, g_first))
+
+            banks, where = before
+            result = work.tile([P, O_TILES, CHUNK], F32, name="result")
+            nc.vector.tensor_scalar(
+                out=result[:, 0, :], in0=banks[0][:], scalar1=br_wide[:, 0:1], scalar2=None, op0=ADD
+            )
+            nc.scalar.activation(
+                out=result[:, 1, :], in_=banks[1][:], func=IDENTITY, bias=br_wide[:, 1:2], scale=1.0
+            )
+            store(result, where[0], where[1])

@@ -17,31 +17,28 @@ K = P * PACK
 O_TILES = O // P
 FRAMES = SAMPLES * T
 G_CHUNK = 8
-CHUNK = G_CHUNK * T
-CHUNKS_PER_SAMPLE = T // G_CHUNK
 
 FLOPS = 2 * 2 * H * C * FRAMES + 2 * O * H * SAMPLES * T * T
 
 
-def load_weight(nc, pool, weight, rows_per_partition, name):
-    rows = pool.tile([P, rows_per_partition * K], BF16, name=name)
-    source = weight.rearrange("(r a) k -> r (a k)", a=rows_per_partition)
-    for first in range(0, rows_per_partition * K, 2 * K):
-        nc.sync.dma_start(out=rows[:, first : first + 2 * K], in_=source[:, first : first + 2 * K])
-    return rows
+def word_view(rows, matrices):
+    return rows[:].bitcast(F32).rearrange("r (m p s) -> r m s p", m=matrices, s=2)
 
 
-def transpose_weight(nc, pool, psum, identity, rows, rows_per_partition, name):
-    words = rows[:].bitcast(F32).rearrange("r (a p s) -> r a s p", a=rows_per_partition, s=2)
-    grouped = pool.tile([P, rows_per_partition * P * PACK], BF16, name=name, align_bytes=64)
-    grouped_words = grouped[:].bitcast(F32).rearrange("p (a r s) -> p a r s", a=rows_per_partition, s=2)
-    for pair in range(rows_per_partition // 2):
-        bank = psum.tile([P, 2, 2, P], F32, name="transposed")
-        for a in range(2):
-            for s in range(2):
-                nc.tensor.transpose(bank[:, a, s, :], words[:, 2 * pair + a, s, :], identity[:])
-        copy = nc.vector.tensor_copy if pair % 2 == 0 else nc.scalar.copy
-        copy(out=grouped_words[:, 2 * pair : 2 * pair + 2], in_=bank[:].rearrange("p a s r -> p a r s"))
+def transpose_pair(nc, psum, identity, words):
+    bank = psum.tile([P, 2, 2, P], F32, name="transposed")
+    for m in range(2):
+        for s in range(2):
+            nc.tensor.transpose(bank[:, m, s, :], words[:, m, s, :], identity[:])
+    return bank
+
+
+def group_pair(nc, pool, bank):
+    grouped = pool.tile([P, 2 * P * PACK], BF16, name="w_grouped", align_bytes=64)
+    nc.vector.tensor_copy(
+        out=grouped[:].bitcast(F32).rearrange("p (m r s) -> p m r s", m=2, s=2),
+        in_=bank[:].rearrange("p m s r -> p m r s"),
+    )
     return grouped
 
 
@@ -51,6 +48,18 @@ def quantise(nc, pool, grouped, name):
     scales = pool.tile([P, columns], U8, name=name + "_scales", align_bytes=64)
     nc.vector.quantize_mx(out=codes[:].bitcast(FP8X4), scales=scales[:], in_=grouped)
     return codes, scales
+
+
+def one_pass(nc, acc, weight, columns, moving):
+    nc.tensor.matmul_mx(
+        out=acc,
+        lhsT=weight[0][:, columns].bitcast(FP8X4),
+        lhsT_scale=weight[1][:, columns],
+        rhs=moving[0][:].bitcast(FP8X4),
+        rhs_scale=moving[1][:],
+        start=True,
+        stop=True,
+    )
 
 
 def load_bias(nc, pool, bias, per_partition, name):
@@ -65,22 +74,41 @@ def widen(nc, pool, raw, name):
     return wide
 
 
+def add_on_vector(nc, result, acc, bias):
+    nc.vector.tensor_scalar(out=result, in0=acc, scalar1=bias, scalar2=None, op0=ADD)
+
+
+def add_on_scalar(nc, result, acc, bias):
+    nc.scalar.activation(out=result, in_=acc, func=IDENTITY, bias=bias, scale=1.0)
+
+
 def tile_ta_block_pa_t_kernel(tc, xm, Wq, bq, Wk, bk, Wr, br, out):
     nc = tc.nc
 
-    def one_pass(acc, weight, columns, moving):
-        nc.tensor.matmul_mx(
-            out=acc,
-            lhsT=weight[0][:, columns].bitcast(FP8X4),
-            lhsT_scale=weight[1][:, columns],
-            rhs=moving[0][:].bitcast(FP8X4),
-            rhs_scale=moving[1][:],
-            start=True,
-            stop=True,
-        )
+    whole = [(n, g_first, G_CHUNK) for n in range(SAMPLES) for g_first in range(0, T, G_CHUNK)]
+    n_last, g_last, g_half = whole[-1][0], whole[-1][1], G_CHUNK // 2
+    chunks = whole[:-1] + [(n_last, g_last, g_half), (n_last, g_last + g_half, g_half)]
 
     with tc.tile_pool(name="keep", bufs=1) as keep, tc.tile_pool(name="work", bufs=3) as work, tc.manual_schedule():
-        with tc.psum_pool(name="head_psum", bufs=4) as head_psum:
+        q_wide = keep.tile([P, PACK, FRAMES], F32)
+        k_wide = keep.tile([P, PACK, FRAMES], F32)
+
+        def new_planes(chunk):
+            return work.tile([P, PACK, chunk[2], T], BF16, name="planes")
+
+        def tanh_plane(planes, chunk, j):
+            n, g_first, g_count = chunk
+            for g in range(g_count):
+                frame = n * T + g_first + g
+                nc.scalar.activation(
+                    out=planes[:, j, g, :],
+                    in_=k_wide[:, j, n * T : (n + 1) * T],
+                    func=TANH,
+                    bias=q_wide[:, j, frame : frame + 1],
+                    scale=-1.0,
+                )
+
+        with tc.psum_pool(name="head_psum", bufs=2) as head_psum:
             bq_raw = load_bias(nc, keep, bq, PACK, "bq_raw")
             bk_raw = load_bias(nc, keep, bk, PACK, "bk_raw")
             br_raw = load_bias(nc, keep, br, O_TILES, "br_raw")
@@ -98,102 +126,86 @@ def tile_ta_block_pa_t_kernel(tc, xm, Wq, bq, Wk, bk, Wr, br, out):
                 out=x_rows[:].rearrange("p n i t -> p n (i t)"),
                 in_=xm.rearrange("n (p i) t -> p n (i t)", i=PACK),
             )
-            wq_rows = load_weight(nc, keep, Wq, PACK, "wq_rows")
-            wk_rows = load_weight(nc, keep, Wk, PACK, "wk_rows")
-            wr_rows = load_weight(nc, keep, Wr, O_TILES, "wr_rows")
+            plane_rows = []
+            for j in range(PACK):
+                rows = keep.tile([P, 2 * K], BF16, name="plane_rows_%d" % j)
+                nc.sync.dma_start(out=rows[:, 0:K], in_=Wq.rearrange("(r j) c -> r j c", j=PACK)[:, j, :])
+                nc.sync.dma_start(out=rows[:, K : 2 * K], in_=Wk.rearrange("(r j) c -> r j c", j=PACK)[:, j, :])
+                plane_rows.append(rows)
+            wr_rows = keep.tile([P, O_TILES * K], BF16)
+            nc.sync.dma_start(out=wr_rows[:], in_=Wr.rearrange("(r a) h -> r (a h)", a=O_TILES))
+            pairs = [word_view(rows, 2) for rows in plane_rows] + [word_view(wr_rows, O_TILES)]
 
             x_grouped = keep.tile([P, SAMPLES, T, PACK], BF16, align_bytes=64)
             nc.vector.tensor_copy(out=x_grouped[:], in_=x_rows[:].rearrange("p n i t -> p n t i"))
             x_mx = quantise(nc, keep, x_grouped[:].rearrange("p n t i -> p (n t i)"), "x")
-
-            wq_grouped = transpose_weight(nc, keep, head_psum, identity, wq_rows, PACK, "wq_grouped")
-            wk_grouped = transpose_weight(nc, keep, head_psum, identity, wk_rows, PACK, "wk_grouped")
-            wq_mx = quantise(nc, keep, wq_grouped[:], "wq")
-            wk_mx = quantise(nc, keep, wk_grouped[:], "wk")
-            wr_grouped = transpose_weight(nc, keep, head_psum, identity, wr_rows, O_TILES, "wr_grouped")
             bq_wide = widen(nc, keep, bq_raw, "bq_wide")
             bk_wide = widen(nc, keep, bk_raw, "bk_wide")
             br_wide = widen(nc, keep, br_raw, "br_wide")
 
-            q_wide = keep.tile([P, PACK, FRAMES], F32)
-            k_wide = keep.tile([P, PACK, FRAMES], F32)
+            first_planes = new_planes(chunks[0])
+            banks = [transpose_pair(nc, head_psum, identity, pairs[0]), transpose_pair(nc, head_psum, identity, pairs[1])]
+            grouped = [group_pair(nc, work, banks[0])]
             for j in range(PACK):
-                heads = slice(j * P, (j + 1) * P)
-                q_acc = head_psum.tile([P, FRAMES], F32, name="q_acc", bufs=2)
-                one_pass(q_acc[:], wq_mx, heads, x_mx)
-                nc.vector.tensor_scalar(
-                    out=q_wide[:, j, :], in0=q_acc[:], scalar1=bq_wide[:, j : j + 1], scalar2=None, op0=ADD
-                )
-                k_acc = head_psum.tile([P, FRAMES], F32, name="k_acc", bufs=2)
-                one_pass(k_acc[:], wk_mx, heads, x_mx)
-                nc.scalar.activation(
-                    out=k_wide[:, j, :], in_=k_acc[:], func=IDENTITY, bias=bk_wide[:, j : j + 1], scale=1.0
-                )
-            wr_mx = quantise(nc, keep, wr_grouped[:], "wr")
+                w_mx = quantise(nc, work, grouped[j][:], "w")
+                q_acc = head_psum.tile([P, FRAMES], F32, name="q_acc")
+                k_acc = head_psum.tile([P, FRAMES], F32, name="k_acc")
+                one_pass(nc, q_acc[:], w_mx, slice(0, P), x_mx)
+                one_pass(nc, k_acc[:], w_mx, slice(P, 2 * P), x_mx)
+                if j + 2 < len(pairs):
+                    banks.append(transpose_pair(nc, head_psum, identity, pairs[j + 2]))
+                grouped.append(group_pair(nc, work, banks[j + 1]))
+                add_on_vector(nc, q_wide[:, j, :], q_acc[:], bq_wide[:, j : j + 1])
+                add_on_scalar(nc, k_wide[:, j, :], k_acc[:], bk_wide[:, j : j + 1])
+                tanh_plane(first_planes, chunks[0], j)
+            wr_mx = quantise(nc, keep, grouped[PACK][:], "wr")
 
         with tc.psum_pool(name="psum", bufs=4) as psum:
 
-            def differences(n, g_first):
-                planes = work.tile([P, PACK, G_CHUNK, T], BF16, name="planes")
-                for j in range(PACK):
-                    for g in range(G_CHUNK):
-                        frame = n * T + g_first + g
-                        nc.scalar.activation(
-                            out=planes[:, j, g, :],
-                            in_=k_wide[:, j, n * T : (n + 1) * T],
-                            func=TANH,
-                            bias=q_wide[:, j, frame : frame + 1],
-                            scale=-1.0,
-                        )
-                return planes
-
-            def regroup(planes):
-                grouped = work.tile([P, CHUNK, PACK], BF16, name="grouped", align_bytes=64)
+            def regroup(planes, chunk):
+                d_grouped = work.tile([P, chunk[2] * T, PACK], BF16, name="d_grouped", align_bytes=64)
                 nc.vector.tensor_copy(
-                    out=grouped[:].rearrange("p (c i) j -> p c j i", i=4),
+                    out=d_grouped[:].rearrange("p (c i) j -> p c j i", i=4),
                     in_=planes[:].rearrange("p j g t -> p j (g t)").rearrange("p j (c i) -> p c j i", i=4),
                 )
-                return grouped
+                return d_grouped
 
-            def mix(d_mx):
-                banks = []
+            def mix(d_mx, chunk):
+                accs = []
                 for a in range(O_TILES):
-                    acc = psum.tile([P, CHUNK], F32, name="acc")
-                    one_pass(acc[:], wr_mx, slice(a * P, (a + 1) * P), d_mx)
-                    banks.append(acc)
-                return banks
+                    acc = psum.tile([P, chunk[2] * T], F32, name="acc")
+                    one_pass(nc, acc[:], wr_mx, slice(a * P, (a + 1) * P), d_mx)
+                    accs.append(acc)
+                return accs
 
-            def store(result, n, g_first):
-                columns = slice(g_first * T, (g_first + G_CHUNK) * T)
+            def store(result, chunk):
+                n, g_first, g_count = chunk
+                columns = slice(g_first * T, (g_first + g_count) * T)
                 nc.sync.dma_start(
                     out=out[n].rearrange("(p a) g t -> p a (g t)", a=O_TILES)[:, :, columns], in_=result[:]
                 )
 
-            chunks = [(n, g_first) for n in range(SAMPLES) for g_first in range(0, T, G_CHUNK)]
-            before = None
-            for n, g_first in chunks:
-                planes = differences(n, g_first)
-                grouped = regroup(planes)
-                if before is not None:
-                    banks, where = before
-                    result = work.tile([P, O_TILES, CHUNK], F32, name="result")
-                    nc.vector.tensor_scalar(
-                        out=result[:, 0, :], in0=banks[0][:], scalar1=br_wide[:, 0:1], scalar2=None, op0=ADD
-                    )
-                d_mx = quantise(nc, work, grouped[:].rearrange("p w j -> p (w j)"), "d")
-                if before is not None:
-                    nc.vector.tensor_scalar(
-                        out=result[:, 1, :], in0=banks[1][:], scalar1=br_wide[:, 1:2], scalar2=None, op0=ADD
-                    )
-                    store(result, where[0], where[1])
-                before = (mix(d_mx), (n, g_first))
+            accs = None
+            for index, chunk in enumerate(chunks):
+                if index == 0:
+                    planes = first_planes
+                else:
+                    planes = new_planes(chunk)
+                    for j in range(PACK):
+                        tanh_plane(planes, chunk, j)
+                add_second = add_on_scalar if index == len(chunks) - 1 else add_on_vector
+                d_grouped = regroup(planes, chunk)
+                if index > 0:
+                    before = chunks[index - 1]
+                    result = work.tile([P, O_TILES, before[2] * T], F32, name="result")
+                    add_on_vector(nc, result[:, 0, :], accs[0][:], br_wide[:, 0:1])
+                d_mx = quantise(nc, work, d_grouped[:].rearrange("p w j -> p (w j)"), "d")
+                if index > 0:
+                    add_second(nc, result[:, 1, :], accs[1][:], br_wide[:, 1:2])
+                    store(result, before)
+                accs = mix(d_mx, chunk)
 
-            banks, where = before
-            result = work.tile([P, O_TILES, CHUNK], F32, name="result")
-            nc.vector.tensor_scalar(
-                out=result[:, 0, :], in0=banks[0][:], scalar1=br_wide[:, 0:1], scalar2=None, op0=ADD
-            )
-            nc.scalar.activation(
-                out=result[:, 1, :], in_=banks[1][:], func=IDENTITY, bias=br_wide[:, 1:2], scale=1.0
-            )
-            store(result, where[0], where[1])
+            result = work.tile([P, O_TILES, chunks[-1][2] * T], F32, name="result")
+            add_on_vector(nc, result[:, 0, :], accs[0][:], br_wide[:, 0:1])
+            add_on_scalar(nc, result[:, 1, :], accs[1][:], br_wide[:, 1:2])
+            store(result, chunks[-1])

@@ -9,6 +9,7 @@ FP8X4 = mybir.dt.float8_e4m3fn_x4
 TANH = mybir.ActivationFunctionType.Tanh
 IDENTITY = mybir.ActivationFunctionType.Identity
 ADD = mybir.AluOpType.add
+SUBTRACT = mybir.AluOpType.subtract
 
 SAMPLES, C, T, H, O = 4, 512, 64, 512, 256
 P = 128
@@ -17,6 +18,7 @@ K = P * PACK
 O_TILES = O // P
 FRAMES = SAMPLES * T
 G_CHUNK = 8
+POOL_SHARE = 4
 
 FLOPS = 2 * 2 * H * C * FRAMES + 2 * O * H * SAMPLES * T * T
 
@@ -94,14 +96,16 @@ def tile_ta_block_pa_t_kernel(tc, xm, Wq, bq, Wk, bk, Wr, br, out):
         k_wide = keep.tile([P, PACK, FRAMES], F32)
 
         def new_planes(chunk):
-            return work.tile([P, PACK, chunk[2], T], BF16, name="planes")
+            g_count = chunk[2]
+            return work.tile([P, PACK, g_count - g_count // POOL_SHARE, T], BF16, name="planes")
 
         def tanh_plane(planes, chunk, j):
             n, g_first, g_count = chunk
-            for g in range(g_count):
+            g_pool = g_count // POOL_SHARE
+            for g in range(g_pool, g_count):
                 frame = n * T + g_first + g
                 nc.scalar.activation(
-                    out=planes[:, j, g, :],
+                    out=planes[:, j, g - g_pool, :],
                     in_=k_wide[:, j, n * T : (n + 1) * T],
                     func=TANH,
                     bias=q_wide[:, j, frame : frame + 1],
@@ -158,17 +162,42 @@ def tile_ta_block_pa_t_kernel(tc, xm, Wq, bq, Wk, bk, Wr, br, out):
                 add_on_vector(nc, q_wide[:, j, :], q_acc[:], bq_wide[:, j : j + 1])
                 add_on_scalar(nc, k_wide[:, j, :], k_acc[:], bk_wide[:, j : j + 1])
                 tanh_plane(first_planes, chunks[0], j)
+            q_inner = keep.tile([P, FRAMES, PACK], F32)
+            k_inner = keep.tile([P, FRAMES, PACK], F32)
+            nc.vector.tensor_copy(out=q_inner[:], in_=q_wide[:].rearrange("p j f -> p f j"))
+            nc.vector.tensor_copy(out=k_inner[:], in_=k_wide[:].rearrange("p j f -> p f j"))
             wr_mx = quantise(nc, keep, grouped[PACK][:], "wr")
 
-        with tc.psum_pool(name="psum", bufs=4) as psum:
+        with tc.psum_pool(name="psum", bufs=6) as psum:
 
-            def regroup(planes, chunk):
-                d_grouped = work.tile([P, chunk[2] * T, PACK], BF16, name="d_grouped", align_bytes=64)
+            def subtract(chunk):
+                n, g_first, g_count = chunk
+                g_pool = g_count // POOL_SHARE
+                first = n * T + g_first
+                shape = [P, g_pool, T, PACK]
+                difference = work.tile(shape, F32, name="difference", bufs=4)
+                nc.gpsimd.tensor_tensor(
+                    out=difference[:],
+                    in0=q_inner[:, first : first + g_pool, :].unsqueeze(2).to_broadcast(shape),
+                    in1=k_inner[:, n * T : (n + 1) * T, :].unsqueeze(1).to_broadcast(shape),
+                    op=SUBTRACT,
+                )
+                return difference
+
+            def regroup(planes, d_grouped):
+                columns = planes.shape[2] * T
                 nc.vector.tensor_copy(
-                    out=d_grouped[:].rearrange("p (c i) j -> p c j i", i=4),
+                    out=d_grouped[:, d_grouped.shape[1] - columns :, :].rearrange("p (c i) j -> p c j i", i=4),
                     in_=planes[:].rearrange("p j g t -> p j (g t)").rearrange("p j (c i) -> p c j i", i=4),
                 )
-                return d_grouped
+
+            def tanh_side_by_side(difference, d_grouped):
+                columns = difference.shape[1] * T
+                nc.scalar.activation(
+                    out=d_grouped[:, 0:columns, :].rearrange("p w j -> p (w j)"),
+                    in_=difference[:].rearrange("p g t j -> p (g t j)"),
+                    func=TANH,
+                )
 
             def mix(d_mx, chunk):
                 accs = []
@@ -185,27 +214,28 @@ def tile_ta_block_pa_t_kernel(tc, xm, Wq, bq, Wk, bk, Wr, br, out):
                     out=out[n].rearrange("(p a) g t -> p a (g t)", a=O_TILES)[:, :, columns], in_=result[:]
                 )
 
-            accs = None
-            for index, chunk in enumerate(chunks):
-                if index == 0:
-                    planes = first_planes
-                else:
-                    planes = new_planes(chunk)
-                    for j in range(PACK):
-                        tanh_plane(planes, chunk, j)
-                add_second = add_on_scalar if index == len(chunks) - 1 else add_on_vector
-                d_grouped = regroup(planes, chunk)
-                if index > 0:
-                    before = chunks[index - 1]
-                    result = work.tile([P, O_TILES, before[2] * T], F32, name="result")
+            differences, d_groupeds, accs_of = [], [], []
+            for step in range(len(chunks) + 2):
+                if step < len(chunks):
+                    chunk = chunks[step]
+                    differences.append(subtract(chunk))
+                    d_groupeds.append(work.tile([P, chunk[2] * T, PACK], BF16, name="d_grouped", align_bytes=64))
+                    if step == 0:
+                        planes = first_planes
+                    else:
+                        planes = new_planes(chunk)
+                        for j in range(PACK):
+                            tanh_plane(planes, chunk, j)
+                    regroup(planes, d_groupeds[step])
+                if 1 <= step <= len(chunks):
+                    tanh_side_by_side(differences[step - 1], d_groupeds[step - 1])
+                    d_mx = quantise(nc, work, d_groupeds[step - 1][:].rearrange("p w j -> p (w j)"), "d")
+                    accs_of.append(mix(d_mx, chunks[step - 1]))
+                if step >= 2:
+                    chunk = chunks[step - 2]
+                    accs = accs_of[step - 2]
+                    add_second = add_on_scalar if step >= len(chunks) else add_on_vector
+                    result = work.tile([P, O_TILES, chunk[2] * T], F32, name="result")
                     add_on_vector(nc, result[:, 0, :], accs[0][:], br_wide[:, 0:1])
-                d_mx = quantise(nc, work, d_grouped[:].rearrange("p w j -> p (w j)"), "d")
-                if index > 0:
                     add_second(nc, result[:, 1, :], accs[1][:], br_wide[:, 1:2])
-                    store(result, before)
-                accs = mix(d_mx, chunk)
-
-            result = work.tile([P, O_TILES, chunks[-1][2] * T], F32, name="result")
-            add_on_vector(nc, result[:, 0, :], accs[0][:], br_wide[:, 0:1])
-            add_on_scalar(nc, result[:, 1, :], accs[1][:], br_wide[:, 1:2])
-            store(result, chunks[-1])
+                    store(result, chunk)

@@ -19,6 +19,7 @@ O_TILES = O // P
 FRAMES = SAMPLES * T
 G_CHUNK = 8
 POOL_SHARE = 4
+EARLY_CHUNKS = 2
 
 FLOPS = 2 * 2 * H * C * FRAMES + 2 * O * H * SAMPLES * T * T
 
@@ -87,21 +88,21 @@ def add_on_scalar(nc, result, acc, bias):
 def tile_ta_block_pa_t_kernel(tc, xm, Wq, bq, Wk, bk, Wr, br, out):
     nc = tc.nc
 
-    whole = [(n, g_first, G_CHUNK) for n in range(SAMPLES) for g_first in range(0, T, G_CHUNK)]
-    n_last, g_last, g_half = whole[-1][0], whole[-1][1], G_CHUNK // 2
-    chunks = whole[:-1] + [(n_last, g_last, g_half), (n_last, g_last + g_half, g_half)]
+    starts = [(n, g_first) for n in range(SAMPLES) for g_first in range(0, T, G_CHUNK)]
+    chunks = [(n, g_first, G_CHUNK, 0) for n, g_first in starts[:EARLY_CHUNKS]]
+    chunks.extend([(n, g_first, G_CHUNK, G_CHUNK // POOL_SHARE) for n, g_first in starts[EARLY_CHUNKS:-1]])
+    n_last, g_last, g_half = starts[-1][0], starts[-1][1], G_CHUNK // 2
+    chunks.extend([(n_last, g_first, g_half, g_half // POOL_SHARE) for g_first in (g_last, g_last + g_half)])
 
     with tc.tile_pool(name="keep", bufs=1) as keep, tc.tile_pool(name="work", bufs=3) as work, tc.manual_schedule():
         q_wide = keep.tile([P, PACK, FRAMES], F32)
         k_wide = keep.tile([P, PACK, FRAMES], F32)
 
         def new_planes(chunk):
-            g_count = chunk[2]
-            return work.tile([P, PACK, g_count - g_count // POOL_SHARE, T], BF16, name="planes")
+            return work.tile([P, PACK, chunk[2] - chunk[3], T], BF16, name="planes")
 
         def tanh_plane(planes, chunk, j):
-            n, g_first, g_count = chunk
-            g_pool = g_count // POOL_SHARE
+            n, g_first, g_count, g_pool = chunk
             for g in range(g_pool, g_count):
                 frame = n * T + g_first + g
                 nc.scalar.activation(
@@ -125,31 +126,33 @@ def tile_ta_block_pa_t_kernel(tc, xm, Wq, bq, Wk, bk, Wr, br, out):
             identity = keep.tile([P, P], F32)
             make_identity(nc, identity[:])
 
+            def load_plane(j):
+                rows = keep.tile([P, 2 * K], BF16, name="plane_rows_%d" % j)
+                nc.sync.dma_start(out=rows[:, 0:K], in_=Wq.rearrange("(r j) c -> r j c", j=PACK)[:, j, :])
+                nc.sync.dma_start(out=rows[:, K : 2 * K], in_=Wk.rearrange("(r j) c -> r j c", j=PACK)[:, j, :])
+                return rows
+
+            plane_rows = [load_plane(0)]
             x_rows = keep.tile([P, SAMPLES, PACK, T], BF16)
             nc.sync.dma_start(
                 out=x_rows[:].rearrange("p n i t -> p n (i t)"),
                 in_=xm.rearrange("n (p i) t -> p n (i t)", i=PACK),
             )
-            plane_rows = []
-            for j in range(PACK):
-                rows = keep.tile([P, 2 * K], BF16, name="plane_rows_%d" % j)
-                nc.sync.dma_start(out=rows[:, 0:K], in_=Wq.rearrange("(r j) c -> r j c", j=PACK)[:, j, :])
-                nc.sync.dma_start(out=rows[:, K : 2 * K], in_=Wk.rearrange("(r j) c -> r j c", j=PACK)[:, j, :])
-                plane_rows.append(rows)
+            plane_rows.extend([load_plane(j) for j in range(1, PACK)])
             wr_rows = keep.tile([P, O_TILES * K], BF16)
             nc.sync.dma_start(out=wr_rows[:], in_=Wr.rearrange("(r a) h -> r (a h)", a=O_TILES))
             pairs = [word_view(rows, 2) for rows in plane_rows] + [word_view(wr_rows, O_TILES)]
 
-            x_grouped = keep.tile([P, SAMPLES, T, PACK], BF16, align_bytes=64)
-            nc.vector.tensor_copy(out=x_grouped[:], in_=x_rows[:].rearrange("p n i t -> p n t i"))
-            x_mx = quantise(nc, keep, x_grouped[:].rearrange("p n t i -> p (n t i)"), "x")
             bq_wide = widen(nc, keep, bq_raw, "bq_wide")
             bk_wide = widen(nc, keep, bk_raw, "bk_wide")
             br_wide = widen(nc, keep, br_raw, "br_wide")
+            x_grouped = keep.tile([P, SAMPLES, T, PACK], BF16, align_bytes=64)
+            nc.scalar.copy(out=x_grouped[:], in_=x_rows[:].rearrange("p n i t -> p n t i"))
 
-            first_planes = new_planes(chunks[0])
+            early_planes = [new_planes(chunk) for chunk in chunks[:EARLY_CHUNKS]]
             banks = [transpose_pair(nc, head_psum, identity, pairs[0]), transpose_pair(nc, head_psum, identity, pairs[1])]
             grouped = [group_pair(nc, work, banks[0])]
+            x_mx = quantise(nc, keep, x_grouped[:].rearrange("p n t i -> p (n t i)"), "x")
             for j in range(PACK):
                 w_mx = quantise(nc, work, grouped[j][:], "w")
                 q_acc = head_psum.tile([P, FRAMES], F32, name="q_acc")
@@ -161,7 +164,8 @@ def tile_ta_block_pa_t_kernel(tc, xm, Wq, bq, Wk, bk, Wr, br, out):
                 grouped.append(group_pair(nc, work, banks[j + 1]))
                 add_on_vector(nc, q_wide[:, j, :], q_acc[:], bq_wide[:, j : j + 1])
                 add_on_scalar(nc, k_wide[:, j, :], k_acc[:], bk_wide[:, j : j + 1])
-                tanh_plane(first_planes, chunks[0], j)
+                for early in range(EARLY_CHUNKS):
+                    tanh_plane(early_planes[early], chunks[early], j)
             q_inner = keep.tile([P, FRAMES, PACK], F32)
             k_inner = keep.tile([P, FRAMES, PACK], F32)
             nc.vector.tensor_copy(out=q_inner[:], in_=q_wide[:].rearrange("p j f -> p f j"))
@@ -171,8 +175,7 @@ def tile_ta_block_pa_t_kernel(tc, xm, Wq, bq, Wk, bk, Wr, br, out):
         with tc.psum_pool(name="psum", bufs=6) as psum:
 
             def subtract(chunk):
-                n, g_first, g_count = chunk
-                g_pool = g_count // POOL_SHARE
+                n, g_first, g_count, g_pool = chunk
                 first = n * T + g_first
                 shape = [P, g_pool, T, PACK]
                 difference = work.tile(shape, F32, name="difference", bufs=4)
@@ -208,7 +211,7 @@ def tile_ta_block_pa_t_kernel(tc, xm, Wq, bq, Wk, bk, Wr, br, out):
                 return accs
 
             def store(result, chunk):
-                n, g_first, g_count = chunk
+                n, g_first, g_count, g_pool = chunk
                 columns = slice(g_first * T, (g_first + g_count) * T)
                 nc.sync.dma_start(
                     out=out[n].rearrange("(p a) g t -> p a (g t)", a=O_TILES)[:, :, columns], in_=result[:]
@@ -218,23 +221,24 @@ def tile_ta_block_pa_t_kernel(tc, xm, Wq, bq, Wk, bk, Wr, br, out):
             for step in range(len(chunks) + 2):
                 if step < len(chunks):
                     chunk = chunks[step]
-                    differences.append(subtract(chunk))
+                    differences.append(subtract(chunk) if chunk[3] > 0 else None)
                     d_groupeds.append(work.tile([P, chunk[2] * T, PACK], BF16, name="d_grouped", align_bytes=64))
-                    if step == 0:
-                        planes = first_planes
+                    if step < EARLY_CHUNKS:
+                        planes = early_planes[step]
                     else:
                         planes = new_planes(chunk)
                         for j in range(PACK):
                             tanh_plane(planes, chunk, j)
                     regroup(planes, d_groupeds[step])
                 if 1 <= step <= len(chunks):
-                    tanh_side_by_side(differences[step - 1], d_groupeds[step - 1])
+                    if differences[step - 1] is not None:
+                        tanh_side_by_side(differences[step - 1], d_groupeds[step - 1])
                     d_mx = quantise(nc, work, d_groupeds[step - 1][:].rearrange("p w j -> p (w j)"), "d")
                     accs_of.append(mix(d_mx, chunks[step - 1]))
                 if step >= 2:
                     chunk = chunks[step - 2]
                     accs = accs_of[step - 2]
-                    add_second = add_on_scalar if step >= len(chunks) else add_on_vector
+                    add_second = add_on_scalar if step >= len(chunks) - 1 else add_on_vector
                     result = work.tile([P, O_TILES, chunk[2] * T], F32, name="result")
                     add_on_vector(nc, result[:, 0, :], accs[0][:], br_wide[:, 0:1])
                     add_second(nc, result[:, 1, :], accs[1][:], br_wide[:, 1:2])

@@ -19,45 +19,47 @@ O_TILES = O // P
 FRAMES = SAMPLES * T
 G_CHUNK = 8
 POOL_SHARE = 4
+POOL_FIRST = 4
 EARLY_CHUNKS = 2
+RUN = 4
 
 FLOPS = 2 * 2 * H * C * FRAMES + 2 * O * H * SAMPLES * T * T
 
 
 def word_view(rows, matrices):
-    return rows[:].bitcast(F32).rearrange("r (m p s) -> r m s p", m=matrices, s=2)
+    return rows[:].bitcast(F32).rearrange("r (b p s) -> r b s p", b=matrices, s=2)
 
 
 def transpose_pair(nc, psum, identity, words):
     bank = psum.tile([P, 2, 2, P], F32, name="transposed")
-    for m in range(2):
+    for b in range(2):
         for s in range(2):
-            nc.tensor.transpose(bank[:, m, s, :], words[:, m, s, :], identity[:])
+            nc.tensor.transpose(bank[:, b, s, :], words[:, b, s, :], identity[:])
     return bank
 
 
 def group_pair(nc, pool, bank):
-    grouped = pool.tile([P, 2 * P * PACK], BF16, name="w_grouped", align_bytes=64)
+    w_grouped = pool.tile([P, 2 * P * PACK], BF16, name="w_grouped", align_bytes=64)
     nc.vector.tensor_copy(
-        out=grouped[:].bitcast(F32).rearrange("p (m r s) -> p m r s", m=2, s=2),
-        in_=bank[:].rearrange("p m s r -> p m r s"),
+        out=w_grouped[:].bitcast(F32).rearrange("p (b r s) -> p b r s", b=2, s=2),
+        in_=bank[:].rearrange("p b s r -> p b r s"),
     )
-    return grouped
+    return w_grouped
 
 
-def quantise(nc, pool, grouped, name):
-    columns = grouped.shape[1] // PACK
-    codes = pool.tile([P, columns], U32, name=name + "_codes", align_bytes=64)
-    scales = pool.tile([P, columns], U8, name=name + "_scales", align_bytes=64)
-    nc.vector.quantize_mx(out=codes[:].bitcast(FP8X4), scales=scales[:], in_=grouped)
+def quantise(nc, pool, values, name):
+    width = values.shape[1] // PACK
+    codes = pool.tile([P, width], U32, name=name + "_codes", align_bytes=64)
+    scales = pool.tile([P, width], U8, name=name + "_scales", align_bytes=64)
+    nc.vector.quantize_mx(out=codes[:].bitcast(FP8X4), scales=scales[:], in_=values)
     return codes, scales
 
 
-def one_pass(nc, acc, weight, columns, moving):
+def one_pass(nc, acc, stationary, columns, moving):
     nc.tensor.matmul_mx(
         out=acc,
-        lhsT=weight[0][:, columns].bitcast(FP8X4),
-        lhsT_scale=weight[1][:, columns],
+        lhsT=stationary[0][:, columns].bitcast(FP8X4),
+        lhsT_scale=stationary[1][:, columns],
         rhs=moving[0][:].bitcast(FP8X4),
         rhs_scale=moving[1][:],
         start=True,
@@ -89,12 +91,12 @@ def tile_ta_block_pa_t_kernel(tc, xm, Wq, bq, Wk, bk, Wr, br, out):
     nc = tc.nc
 
     starts = [(n, g_first) for n in range(SAMPLES) for g_first in range(0, T, G_CHUNK)]
-    chunks = [(n, g_first, G_CHUNK, 0) for n, g_first in starts[:EARLY_CHUNKS]]
-    chunks.extend([(n, g_first, G_CHUNK, G_CHUNK // POOL_SHARE) for n, g_first in starts[EARLY_CHUNKS:-1]])
+    chunks = [(n, g_first, G_CHUNK, 0) for n, g_first in starts[:POOL_FIRST]]
+    chunks.extend([(n, g_first, G_CHUNK, G_CHUNK // POOL_SHARE) for n, g_first in starts[POOL_FIRST:-1]])
     n_last, g_last, g_half = starts[-1][0], starts[-1][1], G_CHUNK // 2
     chunks.extend([(n_last, g_first, g_half, g_half // POOL_SHARE) for g_first in (g_last, g_last + g_half)])
 
-    with tc.tile_pool(name="keep", bufs=1) as keep, tc.tile_pool(name="work", bufs=3) as work, tc.manual_schedule():
+    with tc.tile_pool(name="keep", bufs=1) as keep, tc.tile_pool(name="work", bufs=4) as work, tc.manual_schedule():
         q_wide = keep.tile([P, PACK, FRAMES], F32)
         k_wide = keep.tile([P, PACK, FRAMES], F32)
 
@@ -147,21 +149,21 @@ def tile_ta_block_pa_t_kernel(tc, xm, Wq, bq, Wk, bk, Wr, br, out):
             bk_wide = widen(nc, keep, bk_raw, "bk_wide")
             br_wide = widen(nc, keep, br_raw, "br_wide")
             x_grouped = keep.tile([P, SAMPLES, T, PACK], BF16, align_bytes=64)
-            nc.scalar.copy(out=x_grouped[:], in_=x_rows[:].rearrange("p n i t -> p n t i"))
+            nc.vector.tensor_copy(out=x_grouped[:], in_=x_rows[:].rearrange("p n i t -> p n t i"))
 
             early_planes = [new_planes(chunk) for chunk in chunks[:EARLY_CHUNKS]]
             banks = [transpose_pair(nc, head_psum, identity, pairs[0]), transpose_pair(nc, head_psum, identity, pairs[1])]
-            grouped = [group_pair(nc, work, banks[0])]
+            w_groupeds = [group_pair(nc, work, banks[0])]
             x_mx = quantise(nc, keep, x_grouped[:].rearrange("p n t i -> p (n t i)"), "x")
             for j in range(PACK):
-                w_mx = quantise(nc, work, grouped[j][:], "w")
+                w_mx = quantise(nc, work, w_groupeds[j][:], "w")
                 q_acc = head_psum.tile([P, FRAMES], F32, name="q_acc")
                 k_acc = head_psum.tile([P, FRAMES], F32, name="k_acc")
                 one_pass(nc, q_acc[:], w_mx, slice(0, P), x_mx)
                 one_pass(nc, k_acc[:], w_mx, slice(P, 2 * P), x_mx)
                 if j + 2 < len(pairs):
                     banks.append(transpose_pair(nc, head_psum, identity, pairs[j + 2]))
-                grouped.append(group_pair(nc, work, banks[j + 1]))
+                w_groupeds.append(group_pair(nc, work, banks[j + 1]))
                 add_on_vector(nc, q_wide[:, j, :], q_acc[:], bq_wide[:, j : j + 1])
                 add_on_scalar(nc, k_wide[:, j, :], k_acc[:], bk_wide[:, j : j + 1])
                 for early in range(EARLY_CHUNKS):
@@ -170,34 +172,34 @@ def tile_ta_block_pa_t_kernel(tc, xm, Wq, bq, Wk, bk, Wr, br, out):
             k_inner = keep.tile([P, FRAMES, PACK], F32)
             nc.vector.tensor_copy(out=q_inner[:], in_=q_wide[:].rearrange("p j f -> p f j"))
             nc.vector.tensor_copy(out=k_inner[:], in_=k_wide[:].rearrange("p j f -> p f j"))
-            wr_mx = quantise(nc, keep, grouped[PACK][:], "wr")
+            wr_mx = quantise(nc, keep, w_groupeds[PACK][:], "wr")
 
         with tc.psum_pool(name="psum", bufs=6) as psum:
 
             def subtract(chunk):
-                n, g_first, g_count, g_pool = chunk
-                first = n * T + g_first
+                n, g_first, g_pool = chunk[0], chunk[1], chunk[3]
+                first_frame = n * T + g_first
                 shape = [P, g_pool, T, PACK]
-                difference = work.tile(shape, F32, name="difference", bufs=4)
+                difference = work.tile(shape, F32, name="difference")
                 nc.gpsimd.tensor_tensor(
                     out=difference[:],
-                    in0=q_inner[:, first : first + g_pool, :].unsqueeze(2).to_broadcast(shape),
+                    in0=q_inner[:, first_frame : first_frame + g_pool, :].unsqueeze(2).to_broadcast(shape),
                     in1=k_inner[:, n * T : (n + 1) * T, :].unsqueeze(1).to_broadcast(shape),
                     op=SUBTRACT,
                 )
                 return difference
 
             def regroup(planes, d_grouped):
-                columns = planes.shape[2] * T
+                width = planes.shape[2] * T
                 nc.vector.tensor_copy(
-                    out=d_grouped[:, d_grouped.shape[1] - columns :, :].rearrange("p (c i) j -> p c j i", i=4),
-                    in_=planes[:].rearrange("p j g t -> p j (g t)").rearrange("p j (c i) -> p c j i", i=4),
+                    out=d_grouped[:, d_grouped.shape[1] - width :, :].rearrange("p (u v) j -> p u j v", v=RUN),
+                    in_=planes[:].rearrange("p j g t -> p j (g t)").rearrange("p j (u v) -> p u j v", v=RUN),
                 )
 
             def tanh_side_by_side(difference, d_grouped):
-                columns = difference.shape[1] * T
+                width = difference.shape[1] * T
                 nc.scalar.activation(
-                    out=d_grouped[:, 0:columns, :].rearrange("p w j -> p (w j)"),
+                    out=d_grouped[:, 0:width, :].rearrange("p w j -> p (w j)"),
                     in_=difference[:].rearrange("p g t j -> p (g t j)"),
                     func=TANH,
                 )
@@ -211,7 +213,7 @@ def tile_ta_block_pa_t_kernel(tc, xm, Wq, bq, Wk, bk, Wr, br, out):
                 return accs
 
             def store(result, chunk):
-                n, g_first, g_count, g_pool = chunk
+                n, g_first, g_count = chunk[0], chunk[1], chunk[2]
                 columns = slice(g_first * T, (g_first + g_count) * T)
                 nc.sync.dma_start(
                     out=out[n].rearrange("(p a) g t -> p a (g t)", a=O_TILES)[:, :, columns], in_=result[:]
@@ -239,7 +241,7 @@ def tile_ta_block_pa_t_kernel(tc, xm, Wq, bq, Wk, bk, Wr, br, out):
                     chunk = chunks[step - 2]
                     accs = accs_of[step - 2]
                     add_second = add_on_scalar if step >= len(chunks) - 1 else add_on_vector
-                    result = work.tile([P, O_TILES, chunk[2] * T], F32, name="result")
+                    result = work.tile([P, O_TILES, chunk[2] * T], F32, name="result", bufs=6)
                     add_on_vector(nc, result[:, 0, :], accs[0][:], br_wide[:, 0:1])
                     add_second(nc, result[:, 1, :], accs[1][:], br_wide[:, 1:2])
                     store(result, chunk)

@@ -96,9 +96,10 @@ def tile_ta_block_pa_t_kernel(tc, xm, Wq, bq, Wk, bk, Wr, br, out):
     n_last, g_last, g_half = starts[-1][0], starts[-1][1], G_CHUNK // 2
     chunks.extend([(n_last, g_first, g_half, g_half // POOL_SHARE) for g_first in (g_last, g_last + g_half)])
 
-    with tc.tile_pool(name="keep", bufs=1) as keep, tc.tile_pool(name="work", bufs=4) as work, tc.manual_schedule():
+    with tc.tile_pool(name="keep", bufs=1) as keep, tc.tile_pool(name="work", bufs=4) as work, tc.psum_pool(name="k_psum", bufs=1) as k_psum, tc.manual_schedule():
         q_wide = keep.tile([P, PACK, FRAMES], F32)
         k_wide = keep.tile([P, PACK, FRAMES], F32)
+        k_banks = [k_psum.tile([P, 2, FRAMES], F32, name="k_bank_%d" % b) for b in range(2)]
 
         def new_planes(chunk):
             return work.tile([P, PACK, chunk[2] - chunk[3], T], BF16, name="planes")
@@ -109,7 +110,7 @@ def tile_ta_block_pa_t_kernel(tc, xm, Wq, bq, Wk, bk, Wr, br, out):
                 frame = n * T + g_first + g
                 nc.scalar.activation(
                     out=planes[:, j, g - g_pool, :],
-                    in_=k_wide[:, j, n * T : (n + 1) * T],
+                    in_=k_banks[j % 2][:, j // 2, n * T : (n + 1) * T],
                     func=TANH,
                     bias=q_wide[:, j, frame : frame + 1],
                     scale=-1.0,
@@ -145,8 +146,8 @@ def tile_ta_block_pa_t_kernel(tc, xm, Wq, bq, Wk, bk, Wr, br, out):
             nc.sync.dma_start(out=wr_rows[:], in_=Wr.rearrange("(r a) h -> r (a h)", a=O_TILES))
             pairs = [word_view(rows, 2) for rows in plane_rows] + [word_view(wr_rows, O_TILES)]
 
-            bq_wide = widen(nc, keep, bq_raw, "bq_wide")
-            bk_wide = widen(nc, keep, bk_raw, "bk_wide")
+            bias_wide = keep.tile([P, PACK], F32)
+            nc.vector.tensor_tensor(out=bias_wide[:], in0=bq_raw[:], in1=bk_raw[:], op=SUBTRACT)
             br_wide = widen(nc, keep, br_raw, "br_wide")
             x_grouped = keep.tile([P, SAMPLES, T, PACK], BF16, align_bytes=64)
             nc.vector.tensor_copy(out=x_grouped[:], in_=x_rows[:].rearrange("p n i t -> p n t i"))
@@ -158,16 +159,16 @@ def tile_ta_block_pa_t_kernel(tc, xm, Wq, bq, Wk, bk, Wr, br, out):
             for j in range(PACK):
                 w_mx = quantise(nc, work, w_groupeds[j][:], "w")
                 q_acc = head_psum.tile([P, FRAMES], F32, name="q_acc")
-                k_acc = head_psum.tile([P, FRAMES], F32, name="k_acc")
+                k_acc = k_banks[j % 2][:, j // 2, :]
+                one_pass(nc, k_acc, w_mx, slice(P, 2 * P), x_mx)
                 one_pass(nc, q_acc[:], w_mx, slice(0, P), x_mx)
-                one_pass(nc, k_acc[:], w_mx, slice(P, 2 * P), x_mx)
                 if j + 2 < len(pairs):
                     banks.append(transpose_pair(nc, head_psum, identity, pairs[j + 2]))
                 w_groupeds.append(group_pair(nc, work, banks[j + 1]))
-                add_on_vector(nc, q_wide[:, j, :], q_acc[:], bq_wide[:, j : j + 1])
-                add_on_scalar(nc, k_wide[:, j, :], k_acc[:], bk_wide[:, j : j + 1])
+                add_on_vector(nc, q_wide[:, j, :], q_acc[:], bias_wide[:, j : j + 1])
                 for early in range(EARLY_CHUNKS):
                     tanh_plane(early_planes[early], chunks[early], j)
+                nc.scalar.copy(out=k_wide[:, j, :], in_=k_acc)
             q_inner = keep.tile([P, FRAMES, PACK], F32)
             k_inner = keep.tile([P, FRAMES, PACK], F32)
             nc.vector.tensor_copy(out=q_inner[:], in_=q_wide[:].rearrange("p j f -> p f j"))

@@ -9,6 +9,7 @@ FP8X4 = mybir.dt.float8_e4m3fn_x4
 TANH = mybir.ActivationFunctionType.Tanh
 IDENTITY = mybir.ActivationFunctionType.Identity
 ADD = mybir.AluOpType.add
+MULT = mybir.AluOpType.mult
 SUBTRACT = mybir.AluOpType.subtract
 
 SAMPLES, C, T, H, O = 4, 512, 64, 512, 256
@@ -18,8 +19,15 @@ K = P * PACK
 O_TILES = O // P
 FRAMES = SAMPLES * T
 G_CHUNK = 8
-POOL_SHARE = 4
+POOL_FRAMES = 3
+SCALAR_PAIRS = 1
+HEAD_TURNS = 1
 POOL_FIRST = 4
+PE_FRAMES = 2
+TAIL = ((4, 2), (4, 0))
+SCALAR_BOTH, SCALAR_ONE = 2, 2
+REGROUP_LAG, QUANT_LAG, EMPTY_LAG, POOL_PIECE = 1, 2, 3, 2
+POOL_FROM, POOL_END = 1, 2
 EARLY_CHUNKS = 2
 RUN = 4
 
@@ -38,9 +46,9 @@ def transpose_pair(nc, psum, identity, words):
     return bank
 
 
-def group_pair(nc, pool, bank):
+def group_pair(pool, bank, copy):
     w_grouped = pool.tile([P, 2 * P * PACK], BF16, name="w_grouped", align_bytes=64)
-    nc.vector.tensor_copy(
+    copy(
         out=w_grouped[:].bitcast(F32).rearrange("p (b r s) -> p b r s", b=2, s=2),
         in_=bank[:].rearrange("p b s r -> p b r s"),
     )
@@ -91,28 +99,30 @@ def tile_ta_block_pa_t_kernel(tc, xm, Wq, bq, Wk, bk, Wr, br, out):
     nc = tc.nc
 
     starts = [(n, g_first) for n in range(SAMPLES) for g_first in range(0, T, G_CHUNK)]
-    chunks = [(n, g_first, G_CHUNK, 0) for n, g_first in starts[:POOL_FIRST]]
-    chunks.extend([(n, g_first, G_CHUNK, G_CHUNK // POOL_SHARE) for n, g_first in starts[POOL_FIRST:-1]])
-    n_last, g_last, g_half = starts[-1][0], starts[-1][1], G_CHUNK // 2
-    chunks.extend([(n_last, g_first, g_half, g_half // POOL_SHARE) for g_first in (g_last, g_last + g_half)])
+    chunks = []
+    for i, (n, g_first) in enumerate(starts[:-1]):
+        chunks.append((n, g_first, G_CHUNK, PE_FRAMES if i >= EARLY_CHUNKS and (i + 1) % (T // G_CHUNK) != 0 else 0))
+    g_from = starts[-1][1]
+    for g_count, g_pe in TAIL:
+        chunks.append((SAMPLES - 1, g_from, g_count, g_pe))
+        g_from += g_count
 
-    with tc.tile_pool(name="keep", bufs=1) as keep, tc.tile_pool(name="work", bufs=4) as work, tc.psum_pool(name="k_psum", bufs=1) as k_psum, tc.manual_schedule():
-        q_wide = keep.tile([P, PACK, FRAMES], F32)
-        k_wide = keep.tile([P, PACK, FRAMES], F32)
+    with tc.tile_pool(name="keep", bufs=1) as keep, tc.tile_pool(name="work", bufs=6) as work, tc.psum_pool(name="k_psum", bufs=1) as k_psum, tc.manual_schedule():
+        qk = keep.tile([P, PACK, SAMPLES, 2, T], F32)
         k_banks = [k_psum.tile([P, 2, FRAMES], F32, name="k_bank_%d" % b) for b in range(2)]
 
         def new_planes(chunk):
             return work.tile([P, PACK, chunk[2] - chunk[3], T], BF16, name="planes")
 
         def tanh_plane(planes, chunk, j):
-            n, g_first, g_count, g_pool = chunk
-            for g in range(g_pool, g_count):
-                frame = n * T + g_first + g
+            n, g_first, g_count, g_tensor = chunk
+            for g in range(g_tensor, g_count):
+                frame = g_first + g
                 nc.scalar.activation(
-                    out=planes[:, j, g - g_pool, :],
+                    out=planes[:, j, g - g_tensor, :],
                     in_=k_banks[j % 2][:, j // 2, n * T : (n + 1) * T],
                     func=TANH,
-                    bias=q_wide[:, j, frame : frame + 1],
+                    bias=qk[:, j, n, 0, frame : frame + 1],
                     scale=-1.0,
                 )
 
@@ -128,6 +138,17 @@ def tile_ta_block_pa_t_kernel(tc, xm, Wq, bq, Wk, bk, Wr, br, out):
 
             identity = keep.tile([P, P], F32)
             make_identity(nc, identity[:])
+            slots = T // G_CHUNK
+            selection = keep.tile([P, slots, PE_FRAMES, T], F32)
+            for c in range(slots):
+                g_from = c * G_CHUNK
+                shape = [P, PE_FRAMES, T]
+                nc.gpsimd.tensor_tensor(
+                    out=selection[:, c, :, :],
+                    in0=identity[:, g_from : g_from + PE_FRAMES].unsqueeze(2).to_broadcast(shape),
+                    in1=identity[:, T : 2 * T].unsqueeze(1).to_broadcast(shape),
+                    op=SUBTRACT,
+                )
 
             def load_plane(j):
                 rows = keep.tile([P, 2 * K], BF16, name="plane_rows_%d" % j)
@@ -154,56 +175,88 @@ def tile_ta_block_pa_t_kernel(tc, xm, Wq, bq, Wk, bk, Wr, br, out):
 
             early_planes = [new_planes(chunk) for chunk in chunks[:EARLY_CHUNKS]]
             banks = [transpose_pair(nc, head_psum, identity, pairs[0]), transpose_pair(nc, head_psum, identity, pairs[1])]
-            w_groupeds = [group_pair(nc, work, banks[0])]
+            w_groupeds = [group_pair(work, banks[0], nc.scalar.copy)]
             x_mx = quantise(nc, keep, x_grouped[:].rearrange("p n t i -> p (n t i)"), "x")
+            k_copies = [head_psum.tile([P, 2, FRAMES], F32, name="k_copy_%d" % b, bufs=1) for b in range(2)]
             for j in range(PACK):
                 w_mx = quantise(nc, work, w_groupeds[j][:], "w")
                 q_acc = head_psum.tile([P, FRAMES], F32, name="q_acc")
                 k_acc = k_banks[j % 2][:, j // 2, :]
                 one_pass(nc, k_acc, w_mx, slice(P, 2 * P), x_mx)
                 one_pass(nc, q_acc[:], w_mx, slice(0, P), x_mx)
+                one_pass(nc, k_copies[j // 2][:, j % 2, :], w_mx, slice(P, 2 * P), x_mx)
                 if j + 2 < len(pairs):
                     banks.append(transpose_pair(nc, head_psum, identity, pairs[j + 2]))
-                w_groupeds.append(group_pair(nc, work, banks[j + 1]))
-                add_on_vector(nc, q_wide[:, j, :], q_acc[:], bias_wide[:, j : j + 1])
+                w_groupeds.append(group_pair(work, banks[j + 1], nc.scalar.copy if j + 1 < SCALAR_PAIRS else nc.vector.tensor_copy))
+                add_on_vector(nc, qk[:, j, :, 0, :], q_acc[:].rearrange("p (n t) -> p n t", n=SAMPLES), bias_wide[:, j : j + 1])
                 for early in range(EARLY_CHUNKS):
                     tanh_plane(early_planes[early], chunks[early], j)
-                nc.scalar.copy(out=k_wide[:, j, :], in_=k_acc)
-            q_inner = keep.tile([P, FRAMES, PACK], F32)
-            k_inner = keep.tile([P, FRAMES, PACK], F32)
-            nc.vector.tensor_copy(out=q_inner[:], in_=q_wide[:].rearrange("p j f -> p f j"))
-            nc.vector.tensor_copy(out=k_inner[:], in_=k_wide[:].rearrange("p j f -> p f j"))
+            for b in range(2):
+                for i in range(2):
+                    nc.vector.tensor_copy(
+                        out=qk[:, 2 * b + i, :, 1, :], in_=k_copies[b][:, i, :].rearrange("p (n t) -> p n t", n=SAMPLES)
+                    )
+            def turn_in_head(n):
+                bank = head_psum.tile([P, PACK, P], F32, name="q_acc")
+                for j in range(PACK):
+                    nc.tensor.transpose(bank[:, j, :], qk[:, j, n, :, :].rearrange("p w t -> p (w t)"), identity[:])
+                turned = keep.tile([P, PACK, P], F32, name="turned_%d" % n)
+                nc.vector.tensor_copy(out=turned[:], in_=bank[:])
+                return turned
+            turned_samples = {n: turn_in_head(n) for n in range(HEAD_TURNS)}
             wr_mx = quantise(nc, keep, w_groupeds[PACK][:], "wr")
 
-        with tc.psum_pool(name="psum", bufs=6) as psum:
+        with tc.psum_pool(name="psum", bufs=4) as psum, tc.psum_pool(name="diff_psum", bufs=2) as diff_psum:
 
-            def subtract(chunk):
-                n, g_first, g_pool = chunk[0], chunk[1], chunk[3]
-                first_frame = n * T + g_first
-                shape = [P, g_pool, T, PACK]
-                difference = work.tile(shape, F32, name="difference")
-                nc.gpsimd.tensor_tensor(
-                    out=difference[:],
-                    in0=q_inner[:, first_frame : first_frame + g_pool, :].unsqueeze(2).to_broadcast(shape),
-                    in1=k_inner[:, n * T : (n + 1) * T, :].unsqueeze(1).to_broadcast(shape),
-                    op=SUBTRACT,
-                )
-                return difference
+            def turn_sample(n):
+                bank = diff_psum.tile([P, PACK, P], F32, name="diff")
+                for j in range(PACK):
+                    nc.tensor.transpose(bank[:, j, :], qk[:, j, n, :, :].rearrange("p w t -> p (w t)"), identity[:])
+                return bank
 
-            def regroup(planes, d_grouped):
-                width = planes.shape[2] * T
-                nc.vector.tensor_copy(
-                    out=d_grouped[:, d_grouped.shape[1] - width :, :].rearrange("p (u v) j -> p u j v", v=RUN),
-                    in_=planes[:].rearrange("p j g t -> p j (g t)").rearrange("p j (u v) -> p u j v", v=RUN),
-                )
+            def keep_turned(bank, n):
+                turned = keep.tile([P, PACK, P], F32, name="turned_%d" % n)
+                nc.vector.tensor_copy(out=turned[:], in_=bank[:])
+                return turned
 
-            def tanh_side_by_side(difference, d_grouped):
-                width = difference.shape[1] * T
+            def subtract_on_tensor(chunk):
+                n, g_first = chunk[0], chunk[1]
+                bank = diff_psum.tile([P, PACK, PE_FRAMES * T], F32, name="diff")
+                for j in range(PACK):
+                    nc.tensor.matmul(
+                        bank[:, j, :],
+                        lhsT=turned_samples[n][:, j, :],
+                        rhs=selection[:, g_first // G_CHUNK, :, :].rearrange("p g t -> p (g t)"),
+                        start=True,
+                        stop=True,
+                    )
+                return bank
+
+            def tanh_from_psum(bank, chunk, d_grouped):
                 nc.scalar.activation(
-                    out=d_grouped[:, 0:width, :].rearrange("p w j -> p (w j)"),
-                    in_=difference[:].rearrange("p g t j -> p (g t j)"),
+                    out=d_grouped[:, 0 : PE_FRAMES * T, :],
+                    in_=bank[:].rearrange("p j w -> p w j"),
                     func=TANH,
                 )
+
+            def regroup(planes, d_grouped, frames, engine):
+                behind = d_grouped.shape[1] - planes.shape[2] * T
+                columns = slice(behind + frames.start * T, behind + frames.stop * T)
+                source = planes[:, :, frames, :].rearrange("p j g t -> p j (g t)")
+                if engine == "gpsimd":
+                    nc.gpsimd.tensor_scalar(
+                        out=d_grouped[:, columns, :],
+                        in0=source.rearrange("p j w -> p w j"),
+                        scalar1=1.0,
+                        scalar2=0.0,
+                        op0=MULT,
+                        op1=ADD,
+                    )
+                else:
+                    nc.vector.tensor_copy(
+                        out=d_grouped[:, columns, :].rearrange("p (u v) j -> p u j v", v=RUN),
+                        in_=source.rearrange("p j (u v) -> p u j v", v=RUN),
+                    )
 
             def mix(d_mx, chunk):
                 accs = []
@@ -220,29 +273,57 @@ def tile_ta_block_pa_t_kernel(tc, xm, Wq, bq, Wk, bk, Wr, br, out):
                     out=out[n].rearrange("(p a) g t -> p a (g t)", a=O_TILES)[:, :, columns], in_=result[:]
                 )
 
-            differences, d_groupeds, accs_of = [], [], []
-            for step in range(len(chunks) + 2):
+            d_groupeds, accs_of, pe_banks = [], [], {}
+            turned_banks = {}
+            first_pe_steps, samples_seen = {}, list(turned_samples)
+            for i, chunk in enumerate(chunks):
+                if chunk[3] > 0 and chunk[0] not in samples_seen:
+                    samples_seen.append(chunk[0])
+                    first_pe_steps[i] = chunk[0]
+            all_planes = list(early_planes)
+
+            def pool_frames(i):
+                return POOL_FRAMES if POOL_FROM <= i < len(chunks) - POOL_END else 0
+
+            for step in range(len(chunks) + EMPTY_LAG):
+                if step + 1 in first_pe_steps:
+                    n_turn = first_pe_steps[step + 1]
+                    turned_samples[n_turn] = keep_turned(turned_banks[n_turn], n_turn)
+                if step + 2 in first_pe_steps:
+                    n_turn = first_pe_steps[step + 2]
+                    turned_banks[n_turn] = turn_sample(n_turn)
+                if step + 1 < len(chunks) and chunks[step + 1][3] > 0:
+                    pe_banks[step + 1] = subtract_on_tensor(chunks[step + 1])
                 if step < len(chunks):
                     chunk = chunks[step]
-                    differences.append(subtract(chunk) if chunk[3] > 0 else None)
                     d_groupeds.append(work.tile([P, chunk[2] * T, PACK], BF16, name="d_grouped", align_bytes=64))
-                    if step < EARLY_CHUNKS:
-                        planes = early_planes[step]
-                    else:
-                        planes = new_planes(chunk)
+                    if step >= EARLY_CHUNKS:
+                        all_planes.append(new_planes(chunk))
                         for j in range(PACK):
-                            tanh_plane(planes, chunk, j)
-                    regroup(planes, d_groupeds[step])
-                if 1 <= step <= len(chunks):
-                    if differences[step - 1] is not None:
-                        tanh_side_by_side(differences[step - 1], d_groupeds[step - 1])
-                    d_mx = quantise(nc, work, d_groupeds[step - 1][:].rearrange("p w j -> p (w j)"), "d")
-                    accs_of.append(mix(d_mx, chunks[step - 1]))
-                if step >= 2:
-                    chunk = chunks[step - 2]
-                    accs = accs_of[step - 2]
-                    add_second = add_on_scalar if step >= len(chunks) - 1 else add_on_vector
+                            tanh_plane(all_planes[step], chunk, j)
+                    if step in pe_banks:
+                        tanh_from_psum(pe_banks[step], chunks[step], d_groupeds[step])
+                    g_planes = all_planes[step].shape[2]
+                    g_pool = pool_frames(step)
+                    for g in range(0, g_pool, POOL_PIECE):
+                        regroup(all_planes[step], d_groupeds[step], slice(g, min(g + POOL_PIECE, g_pool)), "gpsimd")
+                i = step - REGROUP_LAG
+                if 0 <= i < len(chunks):
+                    g_planes = all_planes[i].shape[2]
+                    g_pool = pool_frames(i)
+                    regroup(all_planes[i], d_groupeds[i], slice(g_pool, g_planes), "vector")
+                i = step - QUANT_LAG
+                if 0 <= i < len(chunks):
+                    d_mx = quantise(nc, work, d_groupeds[i][:].rearrange("p w j -> p (w j)"), "d")
+                    accs_of.append(mix(d_mx, chunks[i]))
+                i = step - EMPTY_LAG
+                if 0 <= i < len(chunks):
+                    chunk = chunks[i]
+                    accs = accs_of[i]
+                    left = len(chunks) - i
+                    add_second = add_on_scalar if left <= SCALAR_ONE + SCALAR_BOTH else add_on_vector
+                    add_first = add_on_scalar if SCALAR_ONE < left <= SCALAR_ONE + SCALAR_BOTH else add_on_vector
                     result = work.tile([P, O_TILES, chunk[2] * T], F32, name="result", bufs=6)
-                    add_on_vector(nc, result[:, 0, :], accs[0][:], br_wide[:, 0:1])
+                    add_first(nc, result[:, 0, :], accs[0][:], br_wide[:, 0:1])
                     add_second(nc, result[:, 1, :], accs[1][:], br_wide[:, 1:2])
                     store(result, chunk)

@@ -107,9 +107,8 @@ def tile_ta_block_pa_t_kernel(tc, xm, Wq, bq, Wk, bk, Wr, br, out):
         chunks.append((SAMPLES - 1, g_from, g_count, g_pe))
         g_from += g_count
 
-    with tc.tile_pool(name="keep", bufs=1) as keep, tc.tile_pool(name="work", bufs=6) as work, tc.psum_pool(name="k_psum", bufs=1) as k_psum, tc.manual_schedule():
+    with tc.tile_pool(name="keep", bufs=1) as keep, tc.tile_pool(name="work", bufs=6) as work, tc.manual_schedule():
         qk = keep.tile([P, PACK, SAMPLES, 2, T], F32)
-        k_banks = [k_psum.tile([P, 2, FRAMES], F32, name="k_bank_%d" % b) for b in range(2)]
 
         def new_planes(chunk):
             return work.tile([P, PACK, chunk[2] - chunk[3], T], BF16, name="planes")
@@ -120,7 +119,7 @@ def tile_ta_block_pa_t_kernel(tc, xm, Wq, bq, Wk, bk, Wr, br, out):
                 frame = g_first + g
                 nc.scalar.activation(
                     out=planes[:, j, g - g_tensor, :],
-                    in_=k_banks[j % 2][:, j // 2, n * T : (n + 1) * T],
+                    in_=qk[:, j, n, 1, :],
                     func=TANH,
                     bias=qk[:, j, n, 0, frame : frame + 1],
                     scale=-1.0,
@@ -177,25 +176,20 @@ def tile_ta_block_pa_t_kernel(tc, xm, Wq, bq, Wk, bk, Wr, br, out):
             banks = [transpose_pair(nc, head_psum, identity, pairs[0]), transpose_pair(nc, head_psum, identity, pairs[1])]
             w_groupeds = [group_pair(work, banks[0], nc.scalar.copy)]
             x_mx = quantise(nc, keep, x_grouped[:].rearrange("p n t i -> p (n t i)"), "x")
-            k_copies = [head_psum.tile([P, 2, FRAMES], F32, name="k_copy_%d" % b, bufs=1) for b in range(2)]
             for j in range(PACK):
                 w_mx = quantise(nc, work, w_groupeds[j][:], "w")
                 q_acc = head_psum.tile([P, FRAMES], F32, name="q_acc")
-                k_acc = k_banks[j % 2][:, j // 2, :]
-                one_pass(nc, k_acc, w_mx, slice(P, 2 * P), x_mx)
+                k_acc = head_psum.tile([P, FRAMES], F32, name="k_acc")
                 one_pass(nc, q_acc[:], w_mx, slice(0, P), x_mx)
-                one_pass(nc, k_copies[j // 2][:, j % 2, :], w_mx, slice(P, 2 * P), x_mx)
+                one_pass(nc, k_acc[:], w_mx, slice(P, 2 * P), x_mx)
                 if j + 2 < len(pairs):
                     banks.append(transpose_pair(nc, head_psum, identity, pairs[j + 2]))
                 w_groupeds.append(group_pair(work, banks[j + 1], nc.scalar.copy if j + 1 < SCALAR_PAIRS else nc.vector.tensor_copy))
                 add_on_vector(nc, qk[:, j, :, 0, :], q_acc[:].rearrange("p (n t) -> p n t", n=SAMPLES), bias_wide[:, j : j + 1])
+                nc.vector.tensor_copy(out=qk[:, j, :, 1, :], in_=k_acc[:].rearrange("p (n t) -> p n t", n=SAMPLES))
                 for early in range(EARLY_CHUNKS):
                     tanh_plane(early_planes[early], chunks[early], j)
-            for b in range(2):
-                for i in range(2):
-                    nc.vector.tensor_copy(
-                        out=qk[:, 2 * b + i, :, 1, :], in_=k_copies[b][:, i, :].rearrange("p (n t) -> p n t", n=SAMPLES)
-                    )
+
             def turn_in_head(n):
                 bank = head_psum.tile([P, PACK, P], F32, name="q_acc")
                 for j in range(PACK):
@@ -206,7 +200,7 @@ def tile_ta_block_pa_t_kernel(tc, xm, Wq, bq, Wk, bk, Wr, br, out):
             turned_samples = {n: turn_in_head(n) for n in range(HEAD_TURNS)}
             wr_mx = quantise(nc, keep, w_groupeds[PACK][:], "wr")
 
-        with tc.psum_pool(name="psum", bufs=4) as psum, tc.psum_pool(name="diff_psum", bufs=2) as diff_psum:
+        with tc.psum_pool(name="psum", bufs=6) as psum, tc.psum_pool(name="diff_psum", bufs=2) as diff_psum:
 
             def turn_sample(n):
                 bank = diff_psum.tile([P, PACK, P], F32, name="diff")

@@ -19,12 +19,13 @@ K = P * PACK
 O_TILES = O // P
 FRAMES = SAMPLES * T
 G_CHUNK = 8
-POOL_FRAMES = 3
+POOL_FRAMES = 0
 SCALAR_PAIRS = 1
 HEAD_TURNS = 1
-POOL_FIRST = 4
+POOL_FIRST = 3
 PE_FRAMES = 2
-TAIL = ((4, 2), (4, 0))
+TAIL = ((4, 2, 1, 0), (4, 0, 1, 0))
+POOL_SUB, VECTOR_SUB, VECTOR_FIRST, SUB_AHEAD = 2, 0, 4, 3
 SCALAR_BOTH, SCALAR_ONE = 2, 2
 REGROUP_LAG, QUANT_LAG, EMPTY_LAG, POOL_PIECE = 1, 2, 3, 2
 POOL_FROM, POOL_END = 1, 2
@@ -101,24 +102,28 @@ def tile_ta_block_pa_t_kernel(tc, xm, Wq, bq, Wk, bk, Wr, br, out):
     starts = [(n, g_first) for n in range(SAMPLES) for g_first in range(0, T, G_CHUNK)]
     chunks = []
     for i, (n, g_first) in enumerate(starts[:-1]):
-        chunks.append((n, g_first, G_CHUNK, PE_FRAMES if i >= EARLY_CHUNKS and (i + 1) % (T // G_CHUNK) != 0 else 0))
+        g_tensor = PE_FRAMES if i >= EARLY_CHUNKS and (i + 1) % (T // G_CHUNK) != 0 else 0
+        g_pool = POOL_SUB if i >= POOL_FIRST else 0
+        g_vector = VECTOR_SUB if i >= VECTOR_FIRST else 0
+        chunks.append((n, g_first, G_CHUNK, g_tensor, g_pool, g_vector))
     g_from = starts[-1][1]
-    for g_count, g_pe in TAIL:
-        chunks.append((SAMPLES - 1, g_from, g_count, g_pe))
+    for g_count, g_pe, g_pool, g_vector in TAIL:
+        chunks.append((SAMPLES - 1, g_from, g_count, g_pe, g_pool, g_vector))
         g_from += g_count
 
     with tc.tile_pool(name="keep", bufs=1) as keep, tc.tile_pool(name="work", bufs=6) as work, tc.manual_schedule():
         qk = keep.tile([P, PACK, SAMPLES, 2, T], F32)
 
         def new_planes(chunk):
-            return work.tile([P, PACK, chunk[2] - chunk[3], T], BF16, name="planes")
+            return work.tile([P, PACK, chunk[2] - sum(chunk[3:]), T], BF16, name="planes")
 
         def tanh_plane(planes, chunk, j):
-            n, g_first, g_count, g_tensor = chunk
-            for g in range(g_tensor, g_count):
+            n, g_first, g_count = chunk[:3]
+            g_long = sum(chunk[3:])
+            for g in range(g_long, g_count):
                 frame = g_first + g
                 nc.scalar.activation(
-                    out=planes[:, j, g - g_tensor, :],
+                    out=planes[:, j, g - g_long, :],
                     in_=qk[:, j, n, 1, :],
                     func=TANH,
                     bias=qk[:, j, n, 0, frame : frame + 1],
@@ -233,6 +238,38 @@ def tile_ta_block_pa_t_kernel(tc, xm, Wq, bq, Wk, bk, Wr, br, out):
                     func=TANH,
                 )
 
+            qk_inner = keep.tile([P, SAMPLES, 2, T, PACK], F32)
+
+            def side_by_side(n):
+                nc.gpsimd.tensor_scalar(
+                    out=qk_inner[:, n, :, :, :].rearrange("p w t j -> p (w t) j"),
+                    in0=qk[:, :, n, :, :].rearrange("p j w t -> p (w t) j"),
+                    scalar1=1.0,
+                    scalar2=0.0,
+                    op0=MULT,
+                    op1=ADD,
+                )
+
+            def subtract(engine, chunk, difference, g_from, g_count):
+                n = chunk[0]
+                shape = [P, g_count, T, PACK]
+                first = chunk[1] + chunk[3] + g_from
+                engine.tensor_tensor(
+                    out=difference[:, g_from : g_from + g_count, :, :],
+                    in0=qk_inner[:, n, 0, first : first + g_count, :].unsqueeze(2).to_broadcast(shape),
+                    in1=qk_inner[:, n, 1, :, :].unsqueeze(1).to_broadcast(shape),
+                    op=SUBTRACT,
+                )
+
+            def tanh_side_by_side(difference, chunk, d_grouped):
+                first = chunk[3] * T
+                last = first + (chunk[4] + chunk[5]) * T
+                nc.scalar.activation(
+                    out=d_grouped[:, first:last, :].rearrange("p w j -> p (w j)"),
+                    in_=difference[:].rearrange("p g t j -> p (g t j)"),
+                    func=TANH,
+                )
+
             def regroup(planes, d_grouped, frames, engine):
                 behind = d_grouped.shape[1] - planes.shape[2] * T
                 columns = slice(behind + frames.start * T, behind + frames.stop * T)
@@ -279,6 +316,14 @@ def tile_ta_block_pa_t_kernel(tc, xm, Wq, bq, Wk, bk, Wr, br, out):
             def pool_frames(i):
                 return POOL_FRAMES if POOL_FROM <= i < len(chunks) - POOL_END else 0
 
+            differences, inner_done = {}, []
+
+            def difference_of(i):
+                if i not in differences:
+                    chunk = chunks[i]
+                    differences[i] = work.tile([P, chunk[4] + chunk[5], T, PACK], F32, name="difference")
+                return differences[i]
+
             for step in range(len(chunks) + EMPTY_LAG):
                 if step + 1 in first_pe_steps:
                     n_turn = first_pe_steps[step + 1]
@@ -290,6 +335,12 @@ def tile_ta_block_pa_t_kernel(tc, xm, Wq, bq, Wk, bk, Wr, br, out):
                     pe_banks[step + 1] = subtract_on_tensor(chunks[step + 1])
                 if step < len(chunks):
                     chunk = chunks[step]
+                    ahead = min(step + SUB_AHEAD + 1, len(chunks) - 1)
+                    if sum(chunks[ahead][4:]) > 0 and chunks[ahead][0] not in inner_done:
+                        inner_done.append(chunks[ahead][0])
+                        side_by_side(chunks[ahead][0])
+                    if chunk[4] > 0:
+                        subtract(nc.gpsimd, chunk, difference_of(step), 0, chunk[4])
                     d_groupeds.append(work.tile([P, chunk[2] * T, PACK], BF16, name="d_grouped", align_bytes=64))
                     if step >= EARLY_CHUNKS:
                         all_planes.append(new_planes(chunk))
@@ -297,10 +348,15 @@ def tile_ta_block_pa_t_kernel(tc, xm, Wq, bq, Wk, bk, Wr, br, out):
                             tanh_plane(all_planes[step], chunk, j)
                     if step in pe_banks:
                         tanh_from_psum(pe_banks[step], chunks[step], d_groupeds[step])
+                    if step in differences:
+                        tanh_side_by_side(differences[step], chunk, d_groupeds[step])
                     g_planes = all_planes[step].shape[2]
                     g_pool = pool_frames(step)
                     for g in range(0, g_pool, POOL_PIECE):
                         regroup(all_planes[step], d_groupeds[step], slice(g, min(g + POOL_PIECE, g_pool)), "gpsimd")
+                i = step + SUB_AHEAD
+                if i < len(chunks) and chunks[i][5] > 0:
+                    subtract(nc.vector, chunks[i], difference_of(i), chunks[i][4], chunks[i][5])
                 i = step - REGROUP_LAG
                 if 0 <= i < len(chunks):
                     g_planes = all_planes[i].shape[2]

@@ -20,13 +20,13 @@ O_TILES = O // P
 FRAMES = SAMPLES * T
 G_CHUNK = 8
 POOL_FRAMES = 0
-SCALAR_PAIRS = 1
+SCALAR_PAIRS = 2
 HEAD_TURNS = 1
 POOL_FIRST = 3
 PE_FRAMES = 2
 TAIL = ((4, 2, 1, 0), (4, 0, 1, 0))
-POOL_SUB, VECTOR_SUB, VECTOR_FIRST, SUB_AHEAD = 2, 0, 4, 3
-SCALAR_BOTH, SCALAR_ONE = 2, 2
+POOL_SUB, VECTOR_SUB, VECTOR_FIRST = 2, 0, 4
+SCALAR_ONE = 4
 REGROUP_LAG, QUANT_LAG, EMPTY_LAG, POOL_PIECE = 1, 2, 3, 2
 POOL_FROM, POOL_END = 1, 2
 EARLY_CHUNKS = 2
@@ -61,7 +61,7 @@ def quantise(nc, pool, values, name):
     codes = pool.tile([P, width], U32, name=name + "_codes", align_bytes=64)
     scales = pool.tile([P, width], U8, name=name + "_scales", align_bytes=64)
     nc.vector.quantize_mx(out=codes[:].bitcast(FP8X4), scales=scales[:], in_=values)
-    return codes, scales
+    return codes[:], scales[:]
 
 
 def one_pass(nc, acc, stationary, columns, moving):
@@ -69,8 +69,8 @@ def one_pass(nc, acc, stationary, columns, moving):
         out=acc,
         lhsT=stationary[0][:, columns].bitcast(FP8X4),
         lhsT_scale=stationary[1][:, columns],
-        rhs=moving[0][:].bitcast(FP8X4),
-        rhs_scale=moving[1][:],
+        rhs=moving[0].bitcast(FP8X4),
+        rhs_scale=moving[1],
         start=True,
         stop=True,
     )
@@ -131,28 +131,26 @@ def tile_ta_block_pa_t_kernel(tc, xm, Wq, bq, Wk, bk, Wr, br, out):
                 )
 
         with tc.psum_pool(name="head_psum", bufs=2) as head_psum:
-            bq_raw = load_bias(nc, keep, bq, PACK, "bq_raw")
-            bk_raw = load_bias(nc, keep, bk, PACK, "bk_raw")
-            br_raw = load_bias(nc, keep, br, O_TILES, "br_raw")
-
             zero = keep.tile([P, 1], F32)
             nc.vector.memset(zero[:], 0.0)
             unused = keep.tile([P, 1], F32)
             nc.scalar.activation(out=unused[:], in_=zero[:], func=TANH)
+            bq_raw = load_bias(nc, keep, bq, PACK, "bq_raw")
+            bk_raw = load_bias(nc, keep, bk, PACK, "bk_raw")
+            br_raw = load_bias(nc, keep, br, O_TILES, "br_raw")
 
             identity = keep.tile([P, P], F32)
             make_identity(nc, identity[:])
             slots = T // G_CHUNK
             selection = keep.tile([P, slots, PE_FRAMES, T], F32)
-            for c in range(slots):
-                g_from = c * G_CHUNK
-                shape = [P, PE_FRAMES, T]
-                nc.gpsimd.tensor_tensor(
-                    out=selection[:, c, :, :],
-                    in0=identity[:, g_from : g_from + PE_FRAMES].unsqueeze(2).to_broadcast(shape),
-                    in1=identity[:, T : 2 * T].unsqueeze(1).to_broadcast(shape),
-                    op=SUBTRACT,
-                )
+            q_side = identity[:, 0 : slots * G_CHUNK].rearrange("f (c g) -> f c g", g=G_CHUNK)[:, :, 0:PE_FRAMES]
+            k_side = identity[:, T : 2 * T]
+            nc.vector.tensor_tensor(
+                out=selection[:],
+                in0=q_side.unsqueeze(3).to_broadcast([P, slots, PE_FRAMES, T]),
+                in1=k_side.unsqueeze(1).unsqueeze(1).to_broadcast([P, slots, PE_FRAMES, T]),
+                op=SUBTRACT,
+            )
 
             def load_plane(j):
                 rows = keep.tile([P, 2 * K], BF16, name="plane_rows_%d" % j)
@@ -171,32 +169,40 @@ def tile_ta_block_pa_t_kernel(tc, xm, Wq, bq, Wk, bk, Wr, br, out):
             nc.sync.dma_start(out=wr_rows[:], in_=Wr.rearrange("(r a) h -> r (a h)", a=O_TILES))
             pairs = [word_view(rows, 2) for rows in plane_rows] + [word_view(wr_rows, O_TILES)]
 
-            bias_wide = keep.tile([P, PACK], F32)
-            nc.vector.tensor_tensor(out=bias_wide[:], in0=bq_raw[:], in1=bk_raw[:], op=SUBTRACT)
-            br_wide = widen(nc, keep, br_raw, "br_wide")
             x_grouped = keep.tile([P, SAMPLES, T, PACK], BF16, align_bytes=64)
             nc.vector.tensor_copy(out=x_grouped[:], in_=x_rows[:].rearrange("p n i t -> p n t i"))
 
             early_planes = [new_planes(chunk) for chunk in chunks[:EARLY_CHUNKS]]
             banks = [transpose_pair(nc, head_psum, identity, pairs[0]), transpose_pair(nc, head_psum, identity, pairs[1])]
             w_groupeds = [group_pair(work, banks[0], nc.scalar.copy)]
+            w_mxs = [quantise(nc, work, w_groupeds[0][:], "w")]
             x_mx = quantise(nc, keep, x_grouped[:].rearrange("p n t i -> p (n t i)"), "x")
+            bias_wide = keep.tile([P, 2, PACK], F32)
+            nc.vector.tensor_copy(out=bias_wide[:, 0, :], in_=bq_raw[:])
+            nc.vector.tensor_copy(out=bias_wide[:, 1, :], in_=bk_raw[:])
+            br_wide = widen(nc, keep, br_raw, "br_wide")
             for j in range(PACK):
-                w_mx = quantise(nc, work, w_groupeds[j][:], "w")
-                q_acc = head_psum.tile([P, FRAMES], F32, name="q_acc")
-                k_acc = head_psum.tile([P, FRAMES], F32, name="k_acc")
-                one_pass(nc, q_acc[:], w_mx, slice(0, P), x_mx)
-                one_pass(nc, k_acc[:], w_mx, slice(P, 2 * P), x_mx)
+                if j > 0:
+                    w_mxs.append(quantise(nc, work, w_groupeds[j][:], "w"))
+                w_mx = w_mxs[j]
+                qk_acc = head_psum.tile([P, 2, FRAMES], F32, name="qk_acc")
+                one_pass(nc, qk_acc[:, 0, :], w_mx, slice(0, P), x_mx)
+                one_pass(nc, qk_acc[:, 1, :], w_mx, slice(P, 2 * P), x_mx)
                 if j + 2 < len(pairs):
                     banks.append(transpose_pair(nc, head_psum, identity, pairs[j + 2]))
                 w_groupeds.append(group_pair(work, banks[j + 1], nc.scalar.copy if j + 1 < SCALAR_PAIRS else nc.vector.tensor_copy))
-                add_on_vector(nc, qk[:, j, :, 0, :], q_acc[:].rearrange("p (n t) -> p n t", n=SAMPLES), bias_wide[:, j : j + 1])
-                nc.vector.tensor_copy(out=qk[:, j, :, 1, :], in_=k_acc[:].rearrange("p (n t) -> p n t", n=SAMPLES))
+                shape = [P, 2, SAMPLES, T]
+                nc.vector.tensor_tensor(
+                    out=qk[:, j, :, :, :].rearrange("p n w t -> p w n t"),
+                    in0=qk_acc[:].rearrange("p w (n t) -> p w n t", n=SAMPLES),
+                    in1=bias_wide[:, :, j].unsqueeze(2).unsqueeze(3).to_broadcast(shape),
+                    op=ADD,
+                )
                 for early in range(EARLY_CHUNKS):
                     tanh_plane(early_planes[early], chunks[early], j)
 
             def turn_in_head(n):
-                bank = head_psum.tile([P, PACK, P], F32, name="q_acc")
+                bank = head_psum.tile([P, PACK, P], F32, name="qk_acc")
                 for j in range(PACK):
                     nc.tensor.transpose(bank[:, j, :], qk[:, j, n, :, :].rearrange("p w t -> p (w t)"), identity[:])
                 turned = keep.tile([P, PACK, P], F32, name="turned_%d" % n)
@@ -250,12 +256,11 @@ def tile_ta_block_pa_t_kernel(tc, xm, Wq, bq, Wk, bk, Wr, br, out):
                     op1=ADD,
                 )
 
-            def subtract(engine, chunk, difference, g_from, g_count):
-                n = chunk[0]
+            def subtract(chunk, difference):
+                n, first, g_count = chunk[0], chunk[1] + chunk[3], chunk[4]
                 shape = [P, g_count, T, PACK]
-                first = chunk[1] + chunk[3] + g_from
-                engine.tensor_tensor(
-                    out=difference[:, g_from : g_from + g_count, :, :],
+                nc.gpsimd.tensor_tensor(
+                    out=difference[:],
                     in0=qk_inner[:, n, 0, first : first + g_count, :].unsqueeze(2).to_broadcast(shape),
                     in1=qk_inner[:, n, 1, :, :].unsqueeze(1).to_broadcast(shape),
                     op=SUBTRACT,
@@ -318,12 +323,6 @@ def tile_ta_block_pa_t_kernel(tc, xm, Wq, bq, Wk, bk, Wr, br, out):
 
             differences, inner_done = {}, []
 
-            def difference_of(i):
-                if i not in differences:
-                    chunk = chunks[i]
-                    differences[i] = work.tile([P, chunk[4] + chunk[5], T, PACK], F32, name="difference")
-                return differences[i]
-
             for step in range(len(chunks) + EMPTY_LAG):
                 if step + 1 in first_pe_steps:
                     n_turn = first_pe_steps[step + 1]
@@ -335,12 +334,12 @@ def tile_ta_block_pa_t_kernel(tc, xm, Wq, bq, Wk, bk, Wr, br, out):
                     pe_banks[step + 1] = subtract_on_tensor(chunks[step + 1])
                 if step < len(chunks):
                     chunk = chunks[step]
-                    ahead = min(step + SUB_AHEAD + 1, len(chunks) - 1)
-                    if sum(chunks[ahead][4:]) > 0 and chunks[ahead][0] not in inner_done:
-                        inner_done.append(chunks[ahead][0])
-                        side_by_side(chunks[ahead][0])
                     if chunk[4] > 0:
-                        subtract(nc.gpsimd, chunk, difference_of(step), 0, chunk[4])
+                        if chunk[0] not in inner_done:
+                            inner_done.append(chunk[0])
+                            side_by_side(chunk[0])
+                        differences[step] = work.tile([P, chunk[4], T, PACK], F32, name="difference")
+                        subtract(chunk, differences[step])
                     d_groupeds.append(work.tile([P, chunk[2] * T, PACK], BF16, name="d_grouped", align_bytes=64))
                     if step >= EARLY_CHUNKS:
                         all_planes.append(new_planes(chunk))
@@ -354,9 +353,6 @@ def tile_ta_block_pa_t_kernel(tc, xm, Wq, bq, Wk, bk, Wr, br, out):
                     g_pool = pool_frames(step)
                     for g in range(0, g_pool, POOL_PIECE):
                         regroup(all_planes[step], d_groupeds[step], slice(g, min(g + POOL_PIECE, g_pool)), "gpsimd")
-                i = step + SUB_AHEAD
-                if i < len(chunks) and chunks[i][5] > 0:
-                    subtract(nc.vector, chunks[i], difference_of(i), chunks[i][4], chunks[i][5])
                 i = step - REGROUP_LAG
                 if 0 <= i < len(chunks):
                     g_planes = all_planes[i].shape[2]
@@ -371,9 +367,8 @@ def tile_ta_block_pa_t_kernel(tc, xm, Wq, bq, Wk, bk, Wr, br, out):
                     chunk = chunks[i]
                     accs = accs_of[i]
                     left = len(chunks) - i
-                    add_second = add_on_scalar if left <= SCALAR_ONE + SCALAR_BOTH else add_on_vector
-                    add_first = add_on_scalar if SCALAR_ONE < left <= SCALAR_ONE + SCALAR_BOTH else add_on_vector
+                    add_second = add_on_scalar if left <= SCALAR_ONE else add_on_vector
                     result = work.tile([P, O_TILES, chunk[2] * T], F32, name="result", bufs=6)
-                    add_first(nc, result[:, 0, :], accs[0][:], br_wide[:, 0:1])
+                    add_on_vector(nc, result[:, 0, :], accs[0][:], br_wide[:, 0:1])
                     add_second(nc, result[:, 1, :], accs[1][:], br_wide[:, 1:2])
                     store(result, chunk)

@@ -19,16 +19,23 @@ K = P * PACK
 O_TILES = O // P
 FRAMES = SAMPLES * T
 G_CHUNK = 8
-POOL_FRAMES = 0
 SCALAR_PAIRS = 2
-HEAD_TURNS = 1
-POOL_FIRST = 3
+HEAD_TURNS = 2
+POOL_FIRST = 5
 PE_FRAMES = 2
-TAIL = ((4, 2, 1, 0), (4, 0, 1, 0))
-POOL_SUB, VECTOR_SUB, VECTOR_FIRST = 2, 0, 4
 SCALAR_ONE = 4
-REGROUP_LAG, QUANT_LAG, EMPTY_LAG, POOL_PIECE = 1, 2, 3, 2
-POOL_FROM, POOL_END = 1, 2
+REGROUP_LAG, QUANT_LAG, EMPTY_LAG = 1, 2, 3
+SHARES, LAST_SHARES = (2, 2, 1), (1, 1, 1)
+TURNED_FIRST = 5
+TURN_LAG = 3
+K_LAG = 2
+TURN_STEPS = (3, 8)
+LOAD_NUM, LOAD_DEN, LOAD_BASE = 2, 3, 2
+ROW_BUFS = 28
+SUB_AHEAD = 2
+GATE_AHEAD = 2
+INNER_AHEAD = 3
+POOL_PIECE = 1
 EARLY_CHUNKS = 2
 RUN = 4
 
@@ -99,27 +106,36 @@ def add_on_scalar(nc, result, acc, bias):
 def tile_ta_block_pa_t_kernel(tc, xm, Wq, bq, Wk, bk, Wr, br, out):
     nc = tc.nc
 
-    starts = [(n, g_first) for n in range(SAMPLES) for g_first in range(0, T, G_CHUNK)]
     chunks = []
-    for i, (n, g_first) in enumerate(starts[:-1]):
-        g_tensor = PE_FRAMES if i >= EARLY_CHUNKS and (i + 1) % (T // G_CHUNK) != 0 else 0
-        g_pool = POOL_SUB if i >= POOL_FIRST else 0
-        g_vector = VECTOR_SUB if i >= VECTOR_FIRST else 0
-        chunks.append((n, g_first, G_CHUNK, g_tensor, g_pool, g_vector))
-    g_from = starts[-1][1]
-    for g_count, g_pe, g_pool, g_vector in TAIL:
-        chunks.append((SAMPLES - 1, g_from, g_count, g_pe, g_pool, g_vector))
-        g_from += g_count
+    for n in range(SAMPLES):
+        for g_first in range(0, T, G_CHUNK):
+            i = len(chunks)
+            if i < EARLY_CHUNKS:
+                shares = (0, 0, 0)
+            elif i < TURNED_FIRST:
+                shares = (1, 3, 1) if i >= POOL_FIRST else (1, 0, 1)
+            else:
+                shares = SHARES
+            if n == SAMPLES - 1 and g_first == T - G_CHUNK:
+                chunks.append((n, g_first, 4) + LAST_SHARES)
+                chunks.append((n, g_first + 4, 4) + LAST_SHARES)
+            else:
+                chunks.append((n, g_first, G_CHUNK) + shares)
 
-    with tc.tile_pool(name="keep", bufs=1) as keep, tc.tile_pool(name="work", bufs=6) as work, tc.manual_schedule():
+    def planar_frames(chunk):
+        return chunk[2] - PE_FRAMES * chunk[3] - chunk[4] - chunk[5]
+
+    with tc.tile_pool(name="keep", bufs=1) as keep, tc.tile_pool(name="work", bufs=6) as work, tc.psum_pool(name="k_psum", bufs=1) as k_psum, tc.manual_schedule():
         qk = keep.tile([P, PACK, SAMPLES, 2, T], F32)
+        k_banks = [k_psum.tile([P, PACK, 2, T], F32, name="k_bank_%d" % b) for b in range(SAMPLES // 2)]
+        scratch = out[SAMPLES - 1].rearrange("o g t -> (o g t)")[0 : SAMPLES * P * H].rearrange("(r h) -> r h", h=H)
 
         def new_planes(chunk):
-            return work.tile([P, PACK, chunk[2] - sum(chunk[3:]), T], BF16, name="planes")
+            return work.tile([P, PACK, planar_frames(chunk), T], BF16, name="planes")
 
         def tanh_plane(planes, chunk, j):
             n, g_first, g_count = chunk[:3]
-            g_long = sum(chunk[3:])
+            g_long = g_count - planar_frames(chunk)
             for g in range(g_long, g_count):
                 frame = g_first + g
                 nc.scalar.activation(
@@ -127,7 +143,7 @@ def tile_ta_block_pa_t_kernel(tc, xm, Wq, bq, Wk, bk, Wr, br, out):
                     in_=qk[:, j, n, 1, :],
                     func=TANH,
                     bias=qk[:, j, n, 0, frame : frame + 1],
-                    scale=-1.0,
+                    scale=1.0,
                 )
 
         with tc.psum_pool(name="head_psum", bufs=2) as head_psum:
@@ -149,7 +165,7 @@ def tile_ta_block_pa_t_kernel(tc, xm, Wq, bq, Wk, bk, Wr, br, out):
                 out=selection[:],
                 in0=q_side.unsqueeze(3).to_broadcast([P, slots, PE_FRAMES, T]),
                 in1=k_side.unsqueeze(1).unsqueeze(1).to_broadcast([P, slots, PE_FRAMES, T]),
-                op=SUBTRACT,
+                op=ADD,
             )
 
             def load_plane(j):
@@ -177,9 +193,8 @@ def tile_ta_block_pa_t_kernel(tc, xm, Wq, bq, Wk, bk, Wr, br, out):
             w_groupeds = [group_pair(work, banks[0], nc.scalar.copy)]
             w_mxs = [quantise(nc, work, w_groupeds[0][:], "w")]
             x_mx = quantise(nc, keep, x_grouped[:].rearrange("p n t i -> p (n t i)"), "x")
-            bias_wide = keep.tile([P, 2, PACK], F32)
-            nc.vector.tensor_copy(out=bias_wide[:, 0, :], in_=bq_raw[:])
-            nc.vector.tensor_copy(out=bias_wide[:, 1, :], in_=bk_raw[:])
+            bias_wide = keep.tile([P, PACK], F32)
+            nc.vector.tensor_tensor(out=bias_wide[:], in0=bq_raw[:], in1=bk_raw[:], op=SUBTRACT)
             br_wide = widen(nc, keep, br_raw, "br_wide")
             for j in range(PACK):
                 if j > 0:
@@ -191,15 +206,17 @@ def tile_ta_block_pa_t_kernel(tc, xm, Wq, bq, Wk, bk, Wr, br, out):
                 if j + 2 < len(pairs):
                     banks.append(transpose_pair(nc, head_psum, identity, pairs[j + 2]))
                 w_groupeds.append(group_pair(work, banks[j + 1], nc.scalar.copy if j + 1 < SCALAR_PAIRS else nc.vector.tensor_copy))
-                shape = [P, 2, SAMPLES, T]
-                nc.vector.tensor_tensor(
-                    out=qk[:, j, :, :, :].rearrange("p n w t -> p w n t"),
-                    in0=qk_acc[:].rearrange("p w (n t) -> p w n t", n=SAMPLES),
-                    in1=bias_wide[:, :, j].unsqueeze(2).unsqueeze(3).to_broadcast(shape),
-                    op=ADD,
-                )
+                q_acc, k_acc = [qk_acc[:, w, :].rearrange("p (n t) -> p n t", n=SAMPLES) for w in range(2)]
+                add_on_vector(nc, qk[:, j, :, 0, :], q_acc, bias_wide[:, j : j + 1])
+                nc.vector.tensor_scalar(out=qk[:, j, :, 1, :], in0=k_acc, scalar1=-1.0, scalar2=None, op0=MULT)
                 for early in range(EARLY_CHUNKS):
                     tanh_plane(early_planes[early], chunks[early], j)
+
+            for b in range(SAMPLES // 2):
+                pair = slice(b * 2 * T, (b + 1) * 2 * T)
+                x_pair = (x_mx[0][:, pair], x_mx[1][:, pair])
+                for j in range(PACK):
+                    one_pass(nc, k_banks[b][:, j, :, :].rearrange("p n t -> p (n t)"), w_mxs[j], slice(P, 2 * P), x_pair)
 
             def turn_in_head(n):
                 bank = head_psum.tile([P, PACK, P], F32, name="qk_acc")
@@ -211,88 +228,123 @@ def tile_ta_block_pa_t_kernel(tc, xm, Wq, bq, Wk, bk, Wr, br, out):
             turned_samples = {n: turn_in_head(n) for n in range(HEAD_TURNS)}
             wr_mx = quantise(nc, keep, w_groupeds[PACK][:], "wr")
 
-        with tc.psum_pool(name="psum", bufs=6) as psum, tc.psum_pool(name="diff_psum", bufs=2) as diff_psum:
+        with tc.psum_pool(name="psum", bufs=4) as psum, tc.psum_pool(name="diff_psum", bufs=2) as diff_psum:
 
             def turn_sample(n):
-                bank = diff_psum.tile([P, PACK, P], F32, name="diff")
+                bank = psum.tile([P, PACK, P], F32, name="acc")
                 for j in range(PACK):
                     nc.tensor.transpose(bank[:, j, :], qk[:, j, n, :, :].rearrange("p w t -> p (w t)"), identity[:])
-                return bank
+                turned_banks[n] = bank
 
-            def keep_turned(bank, n):
-                turned = keep.tile([P, PACK, P], F32, name="turned_%d" % n)
-                nc.vector.tensor_copy(out=turned[:], in_=bank[:])
-                return turned
+            def keep_turned(n):
+                turned_samples[n] = keep.tile([P, PACK, P], F32, name="turned_%d" % n)
+                nc.vector.tensor_copy(out=turned_samples[n][:], in_=turned_banks[n][:])
 
-            def subtract_on_tensor(chunk):
-                n, g_first = chunk[0], chunk[1]
-                bank = diff_psum.tile([P, PACK, PE_FRAMES * T], F32, name="diff")
-                for j in range(PACK):
-                    nc.tensor.matmul(
-                        bank[:, j, :],
-                        lhsT=turned_samples[n][:, j, :],
-                        rhs=selection[:, g_first // G_CHUNK, :, :].rearrange("p g t -> p (g t)"),
-                        start=True,
-                        stop=True,
-                    )
-                return bank
-
-            def tanh_from_psum(bank, chunk, d_grouped):
-                nc.scalar.activation(
-                    out=d_grouped[:, 0 : PE_FRAMES * T, :],
-                    in_=bank[:].rearrange("p j w -> p w j"),
-                    func=TANH,
+            def park(n):
+                nc.sync.dma_start(
+                    out=scratch[n * P : (n + 1) * P, :], in_=turned_samples[n][:].rearrange("f j h -> f (j h)")
                 )
 
-            qk_inner = keep.tile([P, SAMPLES, 2, T, PACK], F32)
+            def load_k(n):
+                k_rows[n] = keep.tile([P, PACK, P], F32, name="k_rows_%d" % n)
+                for half in range(2):
+                    nc.sync.dma_start(
+                        out=k_rows[n][half * T : (half + 1) * T, :, :].rearrange("f j h -> f (j h)"),
+                        in_=scratch[n * P + T : (n + 1) * P, :],
+                    )
+
+            def plain_planes(chunk, b):
+                if chunk in chunks[:TURNED_FIRST]:
+                    return PACK
+                return 1 if b == 0 and chunk[1] % G_CHUNK == 0 else 0
+
+            def load_rows(chunk):
+                n, g_first = chunk[0], chunk[1]
+                tiles = []
+                for b in range(chunk[3]):
+                    rows = work.tile([P, PACK, P], F32, name="q_rows", bufs=ROW_BUFS)
+                    first = plain_planes(chunk, b)
+                    for half in range(2):
+                        row = n * P + g_first + b * PE_FRAMES + half
+                        nc.sync.dma_start(
+                            out=rows[half * T : (half + 1) * T, first:PACK, :].rearrange("f j h -> f (j h)"),
+                            in_=scratch[row, first * P : PACK * P].partition_broadcast(T),
+                        )
+                    tiles.append(rows)
+                return tiles
+
+            def subtract_on_tensor(i):
+                chunk = chunks[i]
+                n, g_first = chunk[0], chunk[1]
+                banks = []
+                for b in range(chunk[3]):
+                    bank = diff_psum.tile([P, PACK, PE_FRAMES * T], F32, name="diff")
+                    for j in range(PACK):
+                        if j < plain_planes(chunk, b):
+                            nc.tensor.matmul(
+                                bank[:, j, :],
+                                lhsT=turned_samples[n][:, j, :],
+                                rhs=selection[:, g_first // G_CHUNK, :, :].rearrange("p g t -> p (g t)"),
+                                start=True,
+                                stop=True,
+                            )
+                        else:
+                            for rows, first in ((q_rows[i][b], True), (k_rows[n], False)):
+                                nc.tensor.matmul(
+                                    bank[:, j, :],
+                                    lhsT=rows[:, j, :],
+                                    rhs=identity[:],
+                                    is_transpose=True,
+                                    start=first,
+                                    stop=not first,
+                                )
+                    banks.append(bank)
+                return banks
+
+            k_inner = keep.tile([P, SAMPLES, T, PACK], F32)
 
             def side_by_side(n):
                 nc.gpsimd.tensor_scalar(
-                    out=qk_inner[:, n, :, :, :].rearrange("p w t j -> p (w t) j"),
-                    in0=qk[:, :, n, :, :].rearrange("p j w t -> p (w t) j"),
+                    out=k_inner[:, n, :, :],
+                    in0=qk[:, :, n, 1, :].rearrange("p j t -> p t j"),
                     scalar1=1.0,
                     scalar2=0.0,
                     op0=MULT,
                     op1=ADD,
                 )
 
-            def subtract(chunk, difference):
-                n, first, g_count = chunk[0], chunk[1] + chunk[3], chunk[4]
-                shape = [P, g_count, T, PACK]
-                nc.gpsimd.tensor_tensor(
-                    out=difference[:],
-                    in0=qk_inner[:, n, 0, first : first + g_count, :].unsqueeze(2).to_broadcast(shape),
-                    in1=qk_inner[:, n, 1, :, :].unsqueeze(1).to_broadcast(shape),
+            def subtract_on_pool(chunk, difference):
+                n, first = chunk[0], chunk[1] + PE_FRAMES * chunk[3]
+                q_few = work.tile([P, chunk[4], PACK], F32, name="q_few")
+                nc.vector.tensor_copy(
+                    out=q_few[:], in_=qk[:, :, n, 0, first : first + chunk[4]].rearrange("p j g -> p g j")
+                )
+                for g in range(0, chunk[4], POOL_PIECE):
+                    count = min(POOL_PIECE, chunk[4] - g)
+                    shape = [P, count, T, PACK]
+                    nc.gpsimd.tensor_tensor(
+                        out=difference[:, g : g + count, :, :],
+                        in0=q_few[:, g : g + count, :].unsqueeze(2).to_broadcast(shape),
+                        in1=k_inner[:, n, :, :].unsqueeze(1).to_broadcast(shape),
+                        op=ADD,
+                    )
+
+            def subtract_on_vector(chunk, difference):
+                n, first = chunk[0], chunk[1] + PE_FRAMES * chunk[3] + chunk[4]
+                shape = [P, chunk[5], T, PACK]
+                nc.vector.tensor_tensor(
+                    out=difference[:, chunk[4] :, :, :],
+                    in0=qk[:, :, n, 0, first : first + chunk[5]].rearrange("p j g -> p g j").unsqueeze(2).to_broadcast(shape),
+                    in1=k_banks[n // 2][:, :, n % 2, :].rearrange("p j t -> p t j").unsqueeze(1).to_broadcast(shape),
                     op=SUBTRACT,
                 )
 
-            def tanh_side_by_side(difference, chunk, d_grouped):
-                first = chunk[3] * T
-                last = first + (chunk[4] + chunk[5]) * T
-                nc.scalar.activation(
-                    out=d_grouped[:, first:last, :].rearrange("p w j -> p (w j)"),
-                    in_=difference[:].rearrange("p g t j -> p (g t j)"),
-                    func=TANH,
+            def regroup(planes, d_grouped):
+                width = planes.shape[2] * T
+                nc.vector.tensor_copy(
+                    out=d_grouped[:, d_grouped.shape[1] - width :, :].rearrange("p (u v) j -> p u j v", v=RUN),
+                    in_=planes[:].rearrange("p j g t -> p j (g t)").rearrange("p j (u v) -> p u j v", v=RUN),
                 )
-
-            def regroup(planes, d_grouped, frames, engine):
-                behind = d_grouped.shape[1] - planes.shape[2] * T
-                columns = slice(behind + frames.start * T, behind + frames.stop * T)
-                source = planes[:, :, frames, :].rearrange("p j g t -> p j (g t)")
-                if engine == "gpsimd":
-                    nc.gpsimd.tensor_scalar(
-                        out=d_grouped[:, columns, :],
-                        in0=source.rearrange("p j w -> p w j"),
-                        scalar1=1.0,
-                        scalar2=0.0,
-                        op0=MULT,
-                        op1=ADD,
-                    )
-                else:
-                    nc.vector.tensor_copy(
-                        out=d_grouped[:, columns, :].rearrange("p (u v) j -> p u j v", v=RUN),
-                        in_=source.rearrange("p j (u v) -> p u j v", v=RUN),
-                    )
 
             def mix(d_mx, chunk):
                 accs = []
@@ -309,66 +361,76 @@ def tile_ta_block_pa_t_kernel(tc, xm, Wq, bq, Wk, bk, Wr, br, out):
                     out=out[n].rearrange("(p a) g t -> p a (g t)", a=O_TILES)[:, :, columns], in_=result[:]
                 )
 
-            d_groupeds, accs_of, pe_banks = [], [], {}
-            turned_banks = {}
-            first_pe_steps, samples_seen = {}, list(turned_samples)
-            for i, chunk in enumerate(chunks):
-                if chunk[3] > 0 and chunk[0] not in samples_seen:
-                    samples_seen.append(chunk[0])
-                    first_pe_steps[i] = chunk[0]
-            all_planes = list(early_planes)
+            d_groupeds, accs_of, all_planes = [], [], list(early_planes)
+            k_rows, q_rows, pe_banks, differences, inner_done, turned_banks = {}, {}, {}, {}, [], {}
+            for n in range(HEAD_TURNS):
+                park(n)
+            for n in range(HEAD_TURNS):
+                load_k(n)
 
-            def pool_frames(i):
-                return POOL_FRAMES if POOL_FROM <= i < len(chunks) - POOL_END else 0
+            def difference_of(i):
+                if i not in differences:
+                    differences[i] = work.tile([P, chunks[i][4] + chunks[i][5], T, PACK], F32, name="difference")
+                return differences[i]
 
-            differences, inner_done = {}, []
-
+            loaded = TURNED_FIRST
             for step in range(len(chunks) + EMPTY_LAG):
-                if step + 1 in first_pe_steps:
-                    n_turn = first_pe_steps[step + 1]
-                    turned_samples[n_turn] = keep_turned(turned_banks[n_turn], n_turn)
-                if step + 2 in first_pe_steps:
-                    n_turn = first_pe_steps[step + 2]
-                    turned_banks[n_turn] = turn_sample(n_turn)
-                if step + 1 < len(chunks) and chunks[step + 1][3] > 0:
-                    pe_banks[step + 1] = subtract_on_tensor(chunks[step + 1])
+                while loaded < len(chunks) and (LOAD_NUM * loaded) // LOAD_DEN - LOAD_BASE <= step:
+                    q_rows[loaded] = load_rows(chunks[loaded])
+                    loaded += 1
                 if step < len(chunks):
                     chunk = chunks[step]
-                    if chunk[4] > 0:
-                        if chunk[0] not in inner_done:
-                            inner_done.append(chunk[0])
-                            side_by_side(chunk[0])
-                        differences[step] = work.tile([P, chunk[4], T, PACK], F32, name="difference")
-                        subtract(chunk, differences[step])
                     d_groupeds.append(work.tile([P, chunk[2] * T, PACK], BF16, name="d_grouped", align_bytes=64))
-                    if step >= EARLY_CHUNKS:
+                    if step >= EARLY_CHUNKS and planar_frames(chunk) > 0:
                         all_planes.append(new_planes(chunk))
                         for j in range(PACK):
                             tanh_plane(all_planes[step], chunk, j)
-                    if step in pe_banks:
-                        tanh_from_psum(pe_banks[step], chunks[step], d_groupeds[step])
+                    elif step >= EARLY_CHUNKS:
+                        all_planes.append(None)
+                    for b, bank in enumerate(pe_banks.get(step, [])):
+                        nc.scalar.activation(
+                            out=d_groupeds[step][:, b * PE_FRAMES * T : (b + 1) * PE_FRAMES * T, :],
+                            in_=bank[:].rearrange("p j w -> p w j"),
+                            func=TANH,
+                        )
                     if step in differences:
-                        tanh_side_by_side(differences[step], chunk, d_groupeds[step])
-                    g_planes = all_planes[step].shape[2]
-                    g_pool = pool_frames(step)
-                    for g in range(0, g_pool, POOL_PIECE):
-                        regroup(all_planes[step], d_groupeds[step], slice(g, min(g + POOL_PIECE, g_pool)), "gpsimd")
+                        first = PE_FRAMES * chunk[3] * T
+                        nc.scalar.activation(
+                            out=d_groupeds[step][:, first : first + (chunk[4] + chunk[5]) * T, :].rearrange("p w j -> p (w j)"),
+                            in_=differences[step][:].rearrange("p g t j -> p (g t j)"),
+                            func=TANH,
+                        )
+                if step + 1 < len(chunks) and chunks[step + 1][3] > 0:
+                    pe_banks[step + 1] = subtract_on_tensor(step + 1)
                 i = step - REGROUP_LAG
-                if 0 <= i < len(chunks):
-                    g_planes = all_planes[i].shape[2]
-                    g_pool = pool_frames(i)
-                    regroup(all_planes[i], d_groupeds[i], slice(g_pool, g_planes), "vector")
+                if 0 <= i < len(chunks) and all_planes[i] is not None:
+                    regroup(all_planes[i], d_groupeds[i])
+                i = step + GATE_AHEAD
+                if i < len(chunks) and chunks[i][4] > 0:
+                    for n in range(chunks[min(i + INNER_AHEAD, len(chunks) - 1)][0] + 1):
+                        if n not in inner_done:
+                            inner_done.append(n)
+                            side_by_side(n)
+                    subtract_on_pool(chunks[i], difference_of(i))
                 i = step - QUANT_LAG
                 if 0 <= i < len(chunks):
                     d_mx = quantise(nc, work, d_groupeds[i][:].rearrange("p w j -> p (w j)"), "d")
                     accs_of.append(mix(d_mx, chunks[i]))
+                i = step + SUB_AHEAD
+                if i < len(chunks) and chunks[i][5] > 0:
+                    subtract_on_vector(chunks[i], difference_of(i))
+                if step in TURN_STEPS:
+                    turn_sample(TURN_STEPS.index(step) + HEAD_TURNS)
+                if step - TURN_LAG in TURN_STEPS:
+                    keep_turned(TURN_STEPS.index(step - TURN_LAG) + HEAD_TURNS)
+                    park(TURN_STEPS.index(step - TURN_LAG) + HEAD_TURNS)
+                if step - TURN_LAG - K_LAG in TURN_STEPS:
+                    load_k(TURN_STEPS.index(step - TURN_LAG - K_LAG) + HEAD_TURNS)
                 i = step - EMPTY_LAG
                 if 0 <= i < len(chunks):
-                    chunk = chunks[i]
-                    accs = accs_of[i]
                     left = len(chunks) - i
+                    result = work.tile([P, O_TILES, chunks[i][2] * T], F32, name="result", bufs=6)
                     add_second = add_on_scalar if left <= SCALAR_ONE else add_on_vector
-                    result = work.tile([P, O_TILES, chunk[2] * T], F32, name="result", bufs=6)
-                    add_on_vector(nc, result[:, 0, :], accs[0][:], br_wide[:, 0:1])
-                    add_second(nc, result[:, 1, :], accs[1][:], br_wide[:, 1:2])
-                    store(result, chunk)
+                    add_second(nc, result[:, 1, :], accs_of[i][1][:], br_wide[:, 1:2])
+                    add_on_vector(nc, result[:, 0, :], accs_of[i][0][:], br_wide[:, 0:1])
+                    store(result, chunks[i])

@@ -168,6 +168,12 @@ def tile_ta_block_pa_t_kernel(tc, xm, Wq, bq, Wk, bk, Wr, br, out):
                 op=ADD,
             )
 
+            permutation = keep.tile([P, P], F32)
+            nc.vector.tensor_copy(
+                out=permutation[:].rearrange("f (g t) -> f g t", g=PE_FRAMES),
+                in_=identity[:].rearrange("f (t g) -> f g t", g=PE_FRAMES),
+            )
+
             def load_plane(j):
                 rows = keep.tile([P, 2 * K], BF16, name="plane_rows_%d" % j)
                 nc.sync.dma_start(out=rows[:, 0:K], in_=Wq.rearrange("(r j) c -> r j c", j=PACK)[:, j, :])
@@ -247,11 +253,10 @@ def tile_ta_block_pa_t_kernel(tc, xm, Wq, bq, Wk, bk, Wr, br, out):
 
             def load_k(n):
                 k_rows[n] = keep.tile([P, PACK, P], F32, name="k_rows_%d" % n)
-                for half in range(2):
-                    nc.sync.dma_start(
-                        out=k_rows[n][half * T : (half + 1) * T, :, :].rearrange("f j h -> f (j h)"),
-                        in_=scratch[n * P + T : (n + 1) * P, :],
-                    )
+                nc.sync.dma_start(
+                    out=k_rows[n][:].rearrange("f j h -> f (j h)"),
+                    in_=scratch[n * P + T : (n + 1) * P, :].unsqueeze(1).to_broadcast([T, PE_FRAMES, H]),
+                )
 
             def plain_planes(chunk, b):
                 if chunk in chunks[:TURNED_FIRST]:
@@ -264,12 +269,13 @@ def tile_ta_block_pa_t_kernel(tc, xm, Wq, bq, Wk, bk, Wr, br, out):
                 for b in range(chunk[3]):
                     rows = work.tile([P, PACK, P], F32, name="q_rows", bufs=ROW_BUFS)
                     first = plain_planes(chunk, b)
-                    for half in range(2):
-                        row = n * P + g_first + b * PE_FRAMES + half
-                        nc.sync.dma_start(
-                            out=rows[half * T : (half + 1) * T, first:PACK, :].rearrange("f j h -> f (j h)"),
-                            in_=scratch[row, first * P : PACK * P].partition_broadcast(T),
-                        )
+                    row = n * P + g_first + b * PE_FRAMES
+                    nc.sync.dma_start(
+                        out=rows[:, first:PACK, :].rearrange("f j h -> f (j h)"),
+                        in_=scratch[row : row + PE_FRAMES, first * P : PACK * P]
+                        .unsqueeze(0)
+                        .to_broadcast([T, PE_FRAMES, (PACK - first) * P]),
+                    )
                     tiles.append(rows)
                 return tiles
 
@@ -293,7 +299,7 @@ def tile_ta_block_pa_t_kernel(tc, xm, Wq, bq, Wk, bk, Wr, br, out):
                                 nc.tensor.matmul(
                                     bank[:, j, :],
                                     lhsT=rows[:, j, :],
-                                    rhs=identity[:],
+                                    rhs=permutation[:],
                                     is_transpose=True,
                                     start=first,
                                     stop=not first,

@@ -26,12 +26,16 @@ PE_FRAMES = 2
 SCALAR_ONE = 4
 REGROUP_LAG, QUANT_LAG, EMPTY_LAG = 1, 2, 3
 SHARES, LAST_SHARES = (2, 2, 1), (1, 1, 1)
-TURNED_FIRST = 5
+TURNED_FIRST = 6
 TURN_LAG = 3
 K_LAG = 2
-TURN_STEPS = (3, 8)
+TURN_STEPS = (4, 9)
 LOAD_NUM, LOAD_DEN, LOAD_BASE = 2, 3, 2
-ROW_BUFS = 28
+ROW_BUFS = 11
+RESULT_BUFS = 10
+PLAIN = 1
+SINGLE_TURN = 4
+SINGLE_SHARES = (1, 2, 1)
 SUB_AHEAD = 2
 GATE_AHEAD = 2
 INNER_AHEAD = 3
@@ -113,7 +117,9 @@ def tile_ta_block_pa_t_kernel(tc, xm, Wq, bq, Wk, bk, Wr, br, out):
             if i < EARLY_CHUNKS:
                 shares = (0, 0, 0)
             elif i < TURNED_FIRST:
-                shares = (1, 3, 1) if i >= POOL_FIRST else (1, 0, 1)
+                shares = (1, 2, 1) if i >= POOL_FIRST else (1, 0, 1)
+            elif i % SINGLE_TURN == SINGLE_TURN - 1:
+                shares = SINGLE_SHARES
             else:
                 shares = SHARES
             if n == SAMPLES - 1 and g_first == T - G_CHUNK:
@@ -121,6 +127,14 @@ def tile_ta_block_pa_t_kernel(tc, xm, Wq, bq, Wk, bk, Wr, br, out):
                 chunks.append((n, g_first + 4, 4) + LAST_SHARES)
             else:
                 chunks.append((n, g_first, G_CHUNK) + shares)
+
+    def tensor_frames(chunk, b):
+        return (chunk[1] + b, chunk[3])
+
+    def plain_planes(i, b):
+        if chunks[i][3] == 0 or b > 0:
+            return 0
+        return PACK if chunks[i][3] == 1 else PLAIN
 
     def planar_frames(chunk):
         return chunk[2] - PE_FRAMES * chunk[3] - chunk[4] - chunk[5]
@@ -131,7 +145,7 @@ def tile_ta_block_pa_t_kernel(tc, xm, Wq, bq, Wk, bk, Wr, br, out):
         scratch = out[SAMPLES - 1].rearrange("o g t -> (o g t)")[0 : SAMPLES * P * H].rearrange("(r h) -> r h", h=H)
 
         def new_planes(chunk):
-            return work.tile([P, PACK, planar_frames(chunk), T], BF16, name="planes")
+            return work.tile([P, PACK, planar_frames(chunk), T], BF16, name="planes", bufs=4)
 
         def tanh_plane(planes, chunk, j):
             n, g_first, g_count = chunk[:3]
@@ -157,16 +171,19 @@ def tile_ta_block_pa_t_kernel(tc, xm, Wq, bq, Wk, bk, Wr, br, out):
 
             identity = keep.tile([P, P], F32)
             make_identity(nc, identity[:])
-            slots = T // G_CHUNK
-            selection = keep.tile([P, slots, PE_FRAMES, T], F32)
-            q_side = identity[:, 0 : slots * G_CHUNK].rearrange("f (c g) -> f c g", g=G_CHUNK)[:, :, 0:PE_FRAMES]
-            k_side = identity[:, T : 2 * T]
-            nc.vector.tensor_tensor(
-                out=selection[:],
-                in0=q_side.unsqueeze(3).to_broadcast([P, slots, PE_FRAMES, T]),
-                in1=k_side.unsqueeze(1).unsqueeze(1).to_broadcast([P, slots, PE_FRAMES, T]),
-                op=ADD,
-            )
+            selection = {}
+            for i, chunk in enumerate(chunks):
+                pair = tensor_frames(chunk, 0)
+                if plain_planes(i, 0) > 0 and pair not in selection:
+                    shape = [P, PE_FRAMES, T]
+                    selection[pair] = keep.tile(shape, F32, name="selection_%d_%d" % pair)
+                    last = pair[0] + (PE_FRAMES - 1) * pair[1] + 1
+                    nc.vector.tensor_tensor(
+                        out=selection[pair][:],
+                        in0=identity[:, pair[0] : last : pair[1]].unsqueeze(2).to_broadcast(shape),
+                        in1=identity[:, T : 2 * T].unsqueeze(1).to_broadcast(shape),
+                        op=ADD,
+                    )
 
             permutation = keep.tile([P, P], F32)
             nc.vector.tensor_copy(
@@ -258,47 +275,39 @@ def tile_ta_block_pa_t_kernel(tc, xm, Wq, bq, Wk, bk, Wr, br, out):
                     in_=scratch[n * P + T : (n + 1) * P, :].unsqueeze(1).to_broadcast([T, PE_FRAMES, H]),
                 )
 
-            def plain_planes(chunk, b):
-                if chunk in chunks[:TURNED_FIRST]:
-                    return PACK
-                return 1 if b == 0 and chunk[1] % G_CHUNK == 0 else 0
-
             def load_rows(chunk):
-                n, g_first = chunk[0], chunk[1]
-                tiles = []
-                for b in range(chunk[3]):
-                    rows = work.tile([P, PACK, P], F32, name="q_rows", bufs=ROW_BUFS)
-                    first = plain_planes(chunk, b)
-                    row = n * P + g_first + b * PE_FRAMES
-                    nc.sync.dma_start(
-                        out=rows[:, first:PACK, :].rearrange("f j h -> f (j h)"),
-                        in_=scratch[row : row + PE_FRAMES, first * P : PACK * P]
-                        .unsqueeze(0)
-                        .to_broadcast([T, PE_FRAMES, (PACK - first) * P]),
-                    )
-                    tiles.append(rows)
-                return tiles
+                n, g_first, banks = chunk[0], chunk[1], chunk[3]
+                rows = work.tile([P, banks, PACK, P], F32, name="q_rows", bufs=ROW_BUFS)
+                first = n * P + g_first
+                nc.sync.dma_start(
+                    out=rows[:].rearrange("f b j h -> f (b j h)"),
+                    in_=scratch[first : first + banks * PE_FRAMES, :]
+                    .rearrange("(g b) h -> g (b h)", b=banks)
+                    .unsqueeze(0)
+                    .to_broadcast([T, PE_FRAMES, banks * H]),
+                )
+                return rows
 
             def subtract_on_tensor(i):
                 chunk = chunks[i]
-                n, g_first = chunk[0], chunk[1]
+                n = chunk[0]
                 banks = []
                 for b in range(chunk[3]):
                     bank = diff_psum.tile([P, PACK, PE_FRAMES * T], F32, name="diff")
                     for j in range(PACK):
-                        if j < plain_planes(chunk, b):
+                        if j < plain_planes(i, b):
                             nc.tensor.matmul(
                                 bank[:, j, :],
                                 lhsT=turned_samples[n][:, j, :],
-                                rhs=selection[:, g_first // G_CHUNK, :, :].rearrange("p g t -> p (g t)"),
+                                rhs=selection[tensor_frames(chunk, b)][:].rearrange("p g t -> p (g t)"),
                                 start=True,
                                 stop=True,
                             )
                         else:
-                            for rows, first in ((q_rows[i][b], True), (k_rows[n], False)):
+                            for rows, first in ((q_rows[i][:, b, j, :], True), (k_rows[n][:, j, :], False)):
                                 nc.tensor.matmul(
                                     bank[:, j, :],
-                                    lhsT=rows[:, j, :],
+                                    lhsT=rows,
                                     rhs=permutation[:],
                                     is_transpose=True,
                                     start=first,
@@ -376,13 +385,14 @@ def tile_ta_block_pa_t_kernel(tc, xm, Wq, bq, Wk, bk, Wr, br, out):
 
             def difference_of(i):
                 if i not in differences:
-                    differences[i] = work.tile([P, chunks[i][4] + chunks[i][5], T, PACK], F32, name="difference")
+                    differences[i] = work.tile([P, chunks[i][4] + chunks[i][5], T, PACK], F32, name="difference", bufs=5)
                 return differences[i]
 
             loaded = TURNED_FIRST
             for step in range(len(chunks) + EMPTY_LAG):
                 while loaded < len(chunks) and (LOAD_NUM * loaded) // LOAD_DEN - LOAD_BASE <= step:
-                    q_rows[loaded] = load_rows(chunks[loaded])
+                    if plain_planes(loaded, 0) < PACK:
+                        q_rows[loaded] = load_rows(chunks[loaded])
                     loaded += 1
                 if step < len(chunks):
                     chunk = chunks[step]
@@ -394,9 +404,10 @@ def tile_ta_block_pa_t_kernel(tc, xm, Wq, bq, Wk, bk, Wr, br, out):
                     elif step >= EARLY_CHUNKS:
                         all_planes.append(None)
                     for b, bank in enumerate(pe_banks.get(step, [])):
+                        columns = d_groupeds[step][:, 0 : chunk[3] * PE_FRAMES * T, :]
                         nc.scalar.activation(
-                            out=d_groupeds[step][:, b * PE_FRAMES * T : (b + 1) * PE_FRAMES * T, :],
-                            in_=bank[:].rearrange("p j w -> p w j"),
+                            out=columns.rearrange("p (g b t) j -> p b g t j", b=chunk[3], t=T)[:, b],
+                            in_=bank[:].rearrange("p j (g t) -> p g t j", t=T),
                             func=TANH,
                         )
                     if step in differences:
@@ -435,7 +446,7 @@ def tile_ta_block_pa_t_kernel(tc, xm, Wq, bq, Wk, bk, Wr, br, out):
                 i = step - EMPTY_LAG
                 if 0 <= i < len(chunks):
                     left = len(chunks) - i
-                    result = work.tile([P, O_TILES, chunks[i][2] * T], F32, name="result", bufs=6)
+                    result = work.tile([P, O_TILES, chunks[i][2] * T], F32, name="result", bufs=RESULT_BUFS)
                     add_second = add_on_scalar if left <= SCALAR_ONE else add_on_vector
                     add_second(nc, result[:, 1, :], accs_of[i][1][:], br_wide[:, 1:2])
                     add_on_vector(nc, result[:, 0, :], accs_of[i][0][:], br_wide[:, 0:1])

@@ -20,6 +20,7 @@ O_TILES = O // P
 FRAMES = SAMPLES * T
 G_CHUNK = 8
 SCALAR_PAIRS = 2
+HALVES = (slice(0, 2), slice(2, 4))
 HEAD_TURNS = 2
 POOL_FIRST = 5
 PE_FRAMES = 2
@@ -34,7 +35,7 @@ LOAD_NUM, LOAD_DEN, LOAD_BASE = 2, 3, 2
 ROW_BUFS = 11
 RESULT_BUFS = 10
 PLAIN = 1
-SINGLE_TURN = 4
+SINGLE_TURN = 5
 SINGLE_SHARES = (1, 2, 1)
 SUB_AHEAD = 2
 GATE_AHEAD = 2
@@ -117,7 +118,7 @@ def tile_ta_block_pa_t_kernel(tc, xm, Wq, bq, Wk, bk, Wr, br, out):
             if i < EARLY_CHUNKS:
                 shares = (0, 0, 0)
             elif i < TURNED_FIRST:
-                shares = (1, 2, 1) if i >= POOL_FIRST else (1, 0, 1)
+                shares = (1, 2, 1) if i >= POOL_FIRST else (1, 0, 0)
             elif i % SINGLE_TURN == SINGLE_TURN - 1:
                 shares = SINGLE_SHARES
             else:
@@ -199,47 +200,79 @@ def tile_ta_block_pa_t_kernel(tc, xm, Wq, bq, Wk, bk, Wr, br, out):
 
             plane_rows = [load_plane(0)]
             x_rows = keep.tile([P, SAMPLES, PACK, T], BF16)
-            nc.sync.dma_start(
-                out=x_rows[:].rearrange("p n i t -> p n (i t)"),
-                in_=xm.rearrange("n (p i) t -> p n (i t)", i=PACK),
-            )
+            for samples in HALVES:
+                nc.sync.dma_start(
+                    out=x_rows[:, samples, :, :].rearrange("p n i t -> p n (i t)"),
+                    in_=xm[samples, :, :].rearrange("n (p i) t -> p n (i t)", i=PACK),
+                )
             plane_rows.extend([load_plane(j) for j in range(1, PACK)])
             wr_rows = keep.tile([P, O_TILES * K], BF16)
             nc.sync.dma_start(out=wr_rows[:], in_=Wr.rearrange("(r a) h -> r (a h)", a=O_TILES))
             pairs = [word_view(rows, 2) for rows in plane_rows] + [word_view(wr_rows, O_TILES)]
 
             x_grouped = keep.tile([P, SAMPLES, T, PACK], BF16, align_bytes=64)
-            nc.vector.tensor_copy(out=x_grouped[:], in_=x_rows[:].rearrange("p n i t -> p n t i"))
+            x_codes = keep.tile([P, FRAMES], U32, align_bytes=64)
+            x_scales = keep.tile([P, FRAMES], U8, align_bytes=64)
+
+            def group_x(samples):
+                nc.vector.tensor_copy(
+                    out=x_grouped[:, samples, :, :], in_=x_rows[:, samples, :, :].rearrange("p n i t -> p n t i")
+                )
+
+            def quantise_x(samples):
+                frames = slice(samples.start * T, samples.stop * T)
+                nc.vector.quantize_mx(
+                    out=x_codes[:, frames].bitcast(FP8X4),
+                    scales=x_scales[:, frames],
+                    in_=x_grouped[:, samples, :, :].rearrange("p n t i -> p (n t i)"),
+                )
+
+            def project(j, samples):
+                frames = slice(samples.start * T, samples.stop * T)
+                acc = head_psum.tile([P, 2, frames.stop - frames.start], F32, name="qk_acc")
+                for w in range(2):
+                    one_pass(nc, acc[:, w, :], w_mxs[j], slice(w * P, (w + 1) * P), (x_codes[:, frames], x_scales[:, frames]))
+                return acc
+
+            def keep_projection(acc, j, samples):
+                count = samples.stop - samples.start
+                q_acc, k_acc = [acc[:, w, :].rearrange("p (n t) -> p n t", n=count) for w in range(2)]
+                add_on_vector(nc, qk[:, j, samples, 0, :], q_acc, bias_wide[:, j : j + 1])
+                nc.vector.tensor_scalar(out=qk[:, j, samples, 1, :], in0=k_acc, scalar1=-1.0, scalar2=None, op0=MULT)
+
+            group_x(HALVES[0])
+            quantise_x(HALVES[0])
+            group_x(HALVES[1])
 
             early_planes = [new_planes(chunk) for chunk in chunks[:EARLY_CHUNKS]]
             banks = [transpose_pair(nc, head_psum, identity, pairs[0]), transpose_pair(nc, head_psum, identity, pairs[1])]
             w_groupeds = [group_pair(work, banks[0], nc.scalar.copy)]
             w_mxs = [quantise(nc, work, w_groupeds[0][:], "w")]
-            x_mx = quantise(nc, keep, x_grouped[:].rearrange("p n t i -> p (n t i)"), "x")
+            quantise_x(HALVES[1])
+            x_mx = (x_codes, x_scales)
             bias_wide = keep.tile([P, PACK], F32)
             nc.vector.tensor_tensor(out=bias_wide[:], in0=bq_raw[:], in1=bk_raw[:], op=SUBTRACT)
             br_wide = widen(nc, keep, br_raw, "br_wide")
             for j in range(PACK):
                 if j > 0:
                     w_mxs.append(quantise(nc, work, w_groupeds[j][:], "w"))
-                w_mx = w_mxs[j]
-                qk_acc = head_psum.tile([P, 2, FRAMES], F32, name="qk_acc")
-                one_pass(nc, qk_acc[:, 0, :], w_mx, slice(0, P), x_mx)
-                one_pass(nc, qk_acc[:, 1, :], w_mx, slice(P, 2 * P), x_mx)
+                samples = HALVES[0] if j == 0 else slice(0, SAMPLES)
+                acc = project(j, samples)
                 if j + 2 < len(pairs):
                     banks.append(transpose_pair(nc, head_psum, identity, pairs[j + 2]))
                 w_groupeds.append(group_pair(work, banks[j + 1], nc.scalar.copy if j + 1 < SCALAR_PAIRS else nc.vector.tensor_copy))
-                q_acc, k_acc = [qk_acc[:, w, :].rearrange("p (n t) -> p n t", n=SAMPLES) for w in range(2)]
-                add_on_vector(nc, qk[:, j, :, 0, :], q_acc, bias_wide[:, j : j + 1])
-                nc.vector.tensor_scalar(out=qk[:, j, :, 1, :], in0=k_acc, scalar1=-1.0, scalar2=None, op0=MULT)
+                keep_projection(acc, j, samples)
                 for early in range(EARLY_CHUNKS):
                     tanh_plane(early_planes[early], chunks[early], j)
 
+            keep_projection(project(0, HALVES[1]), 0, HALVES[1])
             for b in range(SAMPLES // 2):
                 pair = slice(b * 2 * T, (b + 1) * 2 * T)
                 x_pair = (x_mx[0][:, pair], x_mx[1][:, pair])
                 for j in range(PACK):
                     one_pass(nc, k_banks[b][:, j, :, :].rearrange("p n t -> p (n t)"), w_mxs[j], slice(P, 2 * P), x_pair)
+
+            wr_mx = quantise(nc, keep, w_groupeds[PACK][:], "wr")
 
             def turn_in_head(n):
                 bank = head_psum.tile([P, PACK, P], F32, name="qk_acc")
@@ -249,7 +282,6 @@ def tile_ta_block_pa_t_kernel(tc, xm, Wq, bq, Wk, bk, Wr, br, out):
                 nc.vector.tensor_copy(out=turned[:], in_=bank[:])
                 return turned
             turned_samples = {n: turn_in_head(n) for n in range(HEAD_TURNS)}
-            wr_mx = quantise(nc, keep, w_groupeds[PACK][:], "wr")
 
         with tc.psum_pool(name="psum", bufs=4) as psum, tc.psum_pool(name="diff_psum", bufs=2) as diff_psum:
 

import concourse.mybir as mybir
from concourse.masks import make_identity

F32 = mybir.dt.float32
BF16 = mybir.dt.bfloat16
U32 = mybir.dt.uint32
U8 = mybir.dt.uint8
FP8X4 = mybir.dt.float8_e4m3fn_x4
TANH = mybir.ActivationFunctionType.Tanh
IDENTITY = mybir.ActivationFunctionType.Identity
ADD = mybir.AluOpType.add
MULT = mybir.AluOpType.mult
SUBTRACT = mybir.AluOpType.subtract

SAMPLES, C, T, H, O = 4, 512, 64, 512, 256
P = 128
PACK = 4
K = P * PACK
O_TILES = O // P
FRAMES = SAMPLES * T
G_CHUNK = 8
SCALAR_PAIRS = 2
HALVES = (slice(0, 2), slice(2, 4))
HEAD_TURNS = 2
POOL_FIRST = 5
PE_FRAMES = 2
SCALAR_ONE = 4
REGROUP_LAG, QUANT_LAG, EMPTY_LAG = 1, 2, 3
SHARES, LAST_SHARES = (2, 2, 1), (1, 1, 1)
TURNED_FIRST = 6
TURN_LAG = 3
K_LAG = 2
TURN_STEPS = (4, 9)
LOAD_NUM, LOAD_DEN, LOAD_BASE = 2, 3, 2
ROW_BUFS = 11
RESULT_BUFS = 10
PLAIN = 1
SINGLE_TURN = 5
SINGLE_SHARES = (1, 2, 1)
SUB_AHEAD = 2
GATE_AHEAD = 2
INNER_AHEAD = 3
POOL_PIECE = 1
EARLY_CHUNKS = 2
RUN = 4

FLOPS = 2 * 2 * H * C * FRAMES + 2 * O * H * SAMPLES * T * T


def word_view(rows, matrices):
    return rows[:].bitcast(F32).rearrange("r (b p s) -> r b s p", b=matrices, s=2)


def transpose_pair(nc, psum, identity, words):
    bank = psum.tile([P, 2, 2, P], F32, name="transposed")
    for b in range(2):
        for s in range(2):
            nc.tensor.transpose(bank[:, b, s, :], words[:, b, s, :], identity[:])
    return bank


def group_pair(pool, bank, copy):
    w_grouped = pool.tile([P, 2 * P * PACK], BF16, name="w_grouped", align_bytes=64)
    copy(
        out=w_grouped[:].bitcast(F32).rearrange("p (b r s) -> p b r s", b=2, s=2),
        in_=bank[:].rearrange("p b s r -> p b r s"),
    )
    return w_grouped


def quantise(nc, pool, values, name):
    width = values.shape[1] // PACK
    codes = pool.tile([P, width], U32, name=name + "_codes", align_bytes=64)
    scales = pool.tile([P, width], U8, name=name + "_scales", align_bytes=64)
    nc.vector.quantize_mx(out=codes[:].bitcast(FP8X4), scales=scales[:], in_=values)
    return codes[:], scales[:]


def one_pass(nc, acc, stationary, columns, moving):
    nc.tensor.matmul_mx(
        out=acc,
        lhsT=stationary[0][:, columns].bitcast(FP8X4),
        lhsT_scale=stationary[1][:, columns],
        rhs=moving[0].bitcast(FP8X4),
        rhs_scale=moving[1],
        start=True,
        stop=True,
    )


def load_bias(nc, pool, bias, per_partition, name):
    raw = pool.tile([P, per_partition], BF16, name=name)
    nc.scalar.dma_start(out=raw[:], in_=bias.rearrange("(p a) -> p a", a=per_partition))
    return raw


def widen(nc, pool, raw, name):
    wide = pool.tile([P, raw.shape[1]], F32, name=name)
    nc.vector.tensor_copy(out=wide[:], in_=raw[:])
    return wide


def add_on_vector(nc, result, acc, bias):
    nc.vector.tensor_scalar(out=result, in0=acc, scalar1=bias, scalar2=None, op0=ADD)


def add_on_scalar(nc, result, acc, bias):
    nc.scalar.activation(out=result, in_=acc, func=IDENTITY, bias=bias, scale=1.0)


def tile_ta_block_pa_t_kernel(tc, xm, Wq, bq, Wk, bk, Wr, br, out):
    nc = tc.nc

    chunks = []
    for n in range(SAMPLES):
        for g_first in range(0, T, G_CHUNK):
            i = len(chunks)
            if i < EARLY_CHUNKS:
                shares = (0, 0, 0)
            elif i < TURNED_FIRST:
                shares = (1, 2, 1) if i >= POOL_FIRST else (1, 0, 0)
            elif i % SINGLE_TURN == SINGLE_TURN - 1:
                shares = SINGLE_SHARES
            else:
                shares = SHARES
            if n == SAMPLES - 1 and g_first == T - G_CHUNK:
                chunks.append((n, g_first, 4) + LAST_SHARES)
                chunks.append((n, g_first + 4, 4) + LAST_SHARES)
            else:
                chunks.append((n, g_first, G_CHUNK) + shares)

    def tensor_frames(chunk, b):
        return (chunk[1] + b, chunk[3])

    def plain_planes(i, b):
        if chunks[i][3] == 0 or b > 0:
            return 0
        return PACK if chunks[i][3] == 1 else PLAIN

    def planar_frames(chunk):
        return chunk[2] - PE_FRAMES * chunk[3] - chunk[4] - chunk[5]

    with tc.tile_pool(name="keep", bufs=1) as keep, tc.tile_pool(name="work", bufs=6) as work, tc.psum_pool(name="k_psum", bufs=1) as k_psum, tc.manual_schedule():
        qk = keep.tile([P, PACK, SAMPLES, 2, T], F32)
        k_banks = [k_psum.tile([P, PACK, 2, T], F32, name="k_bank_%d" % b) for b in range(SAMPLES // 2)]
        scratch = out[SAMPLES - 1].rearrange("o g t -> (o g t)")[0 : SAMPLES * P * H].rearrange("(r h) -> r h", h=H)

        def new_planes(chunk):
            return work.tile([P, PACK, planar_frames(chunk), T], BF16, name="planes", bufs=4)

        def tanh_plane(planes, chunk, j):
            n, g_first, g_count = chunk[:3]
            g_long = g_count - planar_frames(chunk)
            for g in range(g_long, g_count):
                frame = g_first + g
                nc.scalar.activation(
                    out=planes[:, j, g - g_long, :],
                    in_=qk[:, j, n, 1, :],
                    func=TANH,
                    bias=qk[:, j, n, 0, frame : frame + 1],
                    scale=1.0,
                )

        with tc.psum_pool(name="head_psum", bufs=2) as head_psum:
            zero = keep.tile([P, 1], F32)
            nc.vector.memset(zero[:], 0.0)
            unused = keep.tile([P, 1], F32)
            nc.scalar.activation(out=unused[:], in_=zero[:], func=TANH)
            bq_raw = load_bias(nc, keep, bq, PACK, "bq_raw")
            bk_raw = load_bias(nc, keep, bk, PACK, "bk_raw")
            br_raw = load_bias(nc, keep, br, O_TILES, "br_raw")

            identity = keep.tile([P, P], F32)
            make_identity(nc, identity[:])
            selection = {}
            for i, chunk in enumerate(chunks):
                pair = tensor_frames(chunk, 0)
                if plain_planes(i, 0) > 0 and pair not in selection:
                    shape = [P, PE_FRAMES, T]
                    selection[pair] = keep.tile(shape, F32, name="selection_%d_%d" % pair)
                    last = pair[0] + (PE_FRAMES - 1) * pair[1] + 1
                    nc.vector.tensor_tensor(
                        out=selection[pair][:],
                        in0=identity[:, pair[0] : last : pair[1]].unsqueeze(2).to_broadcast(shape),
                        in1=identity[:, T : 2 * T].unsqueeze(1).to_broadcast(shape),
                        op=ADD,
                    )

            permutation = keep.tile([P, P], F32)
            nc.vector.tensor_copy(
                out=permutation[:].rearrange("f (g t) -> f g t", g=PE_FRAMES),
                in_=identity[:].rearrange("f (t g) -> f g t", g=PE_FRAMES),
            )

            def load_plane(j):
                rows = keep.tile([P, 2 * K], BF16, name="plane_rows_%d" % j)
                nc.sync.dma_start(out=rows[:, 0:K], in_=Wq.rearrange("(r j) c -> r j c", j=PACK)[:, j, :])
                nc.sync.dma_start(out=rows[:, K : 2 * K], in_=Wk.rearrange("(r j) c -> r j c", j=PACK)[:, j, :])
                return rows

            plane_rows = [load_plane(0)]
            x_rows = keep.tile([P, SAMPLES, PACK, T], BF16)
            for samples in HALVES:
                nc.sync.dma_start(
                    out=x_rows[:, samples, :, :].rearrange("p n i t -> p n (i t)"),
                    in_=xm[samples, :, :].rearrange("n (p i) t -> p n (i t)", i=PACK),
                )
            plane_rows.extend([load_plane(j) for j in range(1, PACK)])
            wr_rows = keep.tile([P, O_TILES * K], BF16)
            nc.sync.dma_start(out=wr_rows[:], in_=Wr.rearrange("(r a) h -> r (a h)", a=O_TILES))
            pairs = [word_view(rows, 2) for rows in plane_rows] + [word_view(wr_rows, O_TILES)]

            x_grouped = keep.tile([P, SAMPLES, T, PACK], BF16, align_bytes=64)
            x_codes = keep.tile([P, FRAMES], U32, align_bytes=64)
            x_scales = keep.tile([P, FRAMES], U8, align_bytes=64)

            def group_x(samples):
                nc.vector.tensor_copy(
                    out=x_grouped[:, samples, :, :], in_=x_rows[:, samples, :, :].rearrange("p n i t -> p n t i")
                )

            def quantise_x(samples):
                frames = slice(samples.start * T, samples.stop * T)
                nc.vector.quantize_mx(
                    out=x_codes[:, frames].bitcast(FP8X4),
                    scales=x_scales[:, frames],
                    in_=x_grouped[:, samples, :, :].rearrange("p n t i -> p (n t i)"),
                )

            def project(j, samples):
                frames = slice(samples.start * T, samples.stop * T)
                acc = head_psum.tile([P, 2, frames.stop - frames.start], F32, name="qk_acc")
                for w in range(2):
                    one_pass(nc, acc[:, w, :], w_mxs[j], slice(w * P, (w + 1) * P), (x_codes[:, frames], x_scales[:, frames]))
                return acc

            def keep_projection(acc, j, samples):
                count = samples.stop - samples.start
                q_acc, k_acc = [acc[:, w, :].rearrange("p (n t) -> p n t", n=count) for w in range(2)]
                add_on_vector(nc, qk[:, j, samples, 0, :], q_acc, bias_wide[:, j : j + 1])
                nc.vector.tensor_scalar(out=qk[:, j, samples, 1, :], in0=k_acc, scalar1=-1.0, scalar2=None, op0=MULT)

            group_x(HALVES[0])
            quantise_x(HALVES[0])
            group_x(HALVES[1])

            early_planes = [new_planes(chunk) for chunk in chunks[:EARLY_CHUNKS]]
            banks = [transpose_pair(nc, head_psum, identity, pairs[0]), transpose_pair(nc, head_psum, identity, pairs[1])]
            w_groupeds = [group_pair(work, banks[0], nc.scalar.copy)]
            w_mxs = [quantise(nc, work, w_groupeds[0][:], "w")]
            quantise_x(HALVES[1])
            x_mx = (x_codes, x_scales)
            bias_wide = keep.tile([P, PACK], F32)
            nc.vector.tensor_tensor(out=bias_wide[:], in0=bq_raw[:], in1=bk_raw[:], op=SUBTRACT)
            br_wide = widen(nc, keep, br_raw, "br_wide")
            for j in range(PACK):
                if j > 0:
                    w_mxs.append(quantise(nc, work, w_groupeds[j][:], "w"))
                samples = HALVES[0] if j == 0 else slice(0, SAMPLES)
                acc = project(j, samples)
                if j + 2 < len(pairs):
                    banks.append(transpose_pair(nc, head_psum, identity, pairs[j + 2]))
                w_groupeds.append(group_pair(work, banks[j + 1], nc.scalar.copy if j + 1 < SCALAR_PAIRS else nc.vector.tensor_copy))
                keep_projection(acc, j, samples)
                for early in range(EARLY_CHUNKS):
                    tanh_plane(early_planes[early], chunks[early], j)

            keep_projection(project(0, HALVES[1]), 0, HALVES[1])
            for b in range(SAMPLES // 2):
                pair = slice(b * 2 * T, (b + 1) * 2 * T)
                x_pair = (x_mx[0][:, pair], x_mx[1][:, pair])
                for j in range(PACK):
                    one_pass(nc, k_banks[b][:, j, :, :].rearrange("p n t -> p (n t)"), w_mxs[j], slice(P, 2 * P), x_pair)

            wr_mx = quantise(nc, keep, w_groupeds[PACK][:], "wr")

            def turn_in_head(n):
                bank = head_psum.tile([P, PACK, P], F32, name="qk_acc")
                for j in range(PACK):
                    nc.tensor.transpose(bank[:, j, :], qk[:, j, n, :, :].rearrange("p w t -> p (w t)"), identity[:])
                turned = keep.tile([P, PACK, P], F32, name="turned_%d" % n)
                nc.vector.tensor_copy(out=turned[:], in_=bank[:])
                return turned
            turned_samples = {n: turn_in_head(n) for n in range(HEAD_TURNS)}

        with tc.psum_pool(name="psum", bufs=4) as psum, tc.psum_pool(name="diff_psum", bufs=2) as diff_psum:

            def turn_sample(n):
                bank = psum.tile([P, PACK, P], F32, name="acc")
                for j in range(PACK):
                    nc.tensor.transpose(bank[:, j, :], qk[:, j, n, :, :].rearrange("p w t -> p (w t)"), identity[:])
                turned_banks[n] = bank

            def keep_turned(n):
                turned_samples[n] = keep.tile([P, PACK, P], F32, name="turned_%d" % n)
                nc.vector.tensor_copy(out=turned_samples[n][:], in_=turned_banks[n][:])

            def park(n):
                nc.sync.dma_start(
                    out=scratch[n * P : (n + 1) * P, :], in_=turned_samples[n][:].rearrange("f j h -> f (j h)")
                )

            def load_k(n):
                k_rows[n] = keep.tile([P, PACK, P], F32, name="k_rows_%d" % n)
                nc.sync.dma_start(
                    out=k_rows[n][:].rearrange("f j h -> f (j h)"),
                    in_=scratch[n * P + T : (n + 1) * P, :].unsqueeze(1).to_broadcast([T, PE_FRAMES, H]),
                )

            def load_rows(chunk):
                n, g_first, banks = chunk[0], chunk[1], chunk[3]
                rows = work.tile([P, banks, PACK, P], F32, name="q_rows", bufs=ROW_BUFS)
                first = n * P + g_first
                nc.sync.dma_start(
                    out=rows[:].rearrange("f b j h -> f (b j h)"),
                    in_=scratch[first : first + banks * PE_FRAMES, :]
                    .rearrange("(g b) h -> g (b h)", b=banks)
                    .unsqueeze(0)
                    .to_broadcast([T, PE_FRAMES, banks * H]),
                )
                return rows

            def subtract_on_tensor(i):
                chunk = chunks[i]
                n = chunk[0]
                banks = []
                for b in range(chunk[3]):
                    bank = diff_psum.tile([P, PACK, PE_FRAMES * T], F32, name="diff")
                    for j in range(PACK):
                        if j < plain_planes(i, b):
                            nc.tensor.matmul(
                                bank[:, j, :],
                                lhsT=turned_samples[n][:, j, :],
                                rhs=selection[tensor_frames(chunk, b)][:].rearrange("p g t -> p (g t)"),
                                start=True,
                                stop=True,
                            )
                        else:
                            for rows, first in ((q_rows[i][:, b, j, :], True), (k_rows[n][:, j, :], False)):
                                nc.tensor.matmul(
                                    bank[:, j, :],
                                    lhsT=rows,
                                    rhs=permutation[:],
                                    is_transpose=True,
                                    start=first,
                                    stop=not first,
                                )
                    banks.append(bank)
                return banks

            k_inner = keep.tile([P, SAMPLES, T, PACK], F32)

            def side_by_side(n):
                nc.gpsimd.tensor_scalar(
                    out=k_inner[:, n, :, :],
                    in0=qk[:, :, n, 1, :].rearrange("p j t -> p t j"),
                    scalar1=1.0,
                    scalar2=0.0,
                    op0=MULT,
                    op1=ADD,
                )

            def subtract_on_pool(chunk, difference):
                n, first = chunk[0], chunk[1] + PE_FRAMES * chunk[3]
                q_few = work.tile([P, chunk[4], PACK], F32, name="q_few")
                nc.vector.tensor_copy(
                    out=q_few[:], in_=qk[:, :, n, 0, first : first + chunk[4]].rearrange("p j g -> p g j")
                )
                for g in range(0, chunk[4], POOL_PIECE):
                    count = min(POOL_PIECE, chunk[4] - g)
                    shape = [P, count, T, PACK]
                    nc.gpsimd.tensor_tensor(
                        out=difference[:, g : g + count, :, :],
                        in0=q_few[:, g : g + count, :].unsqueeze(2).to_broadcast(shape),
                        in1=k_inner[:, n, :, :].unsqueeze(1).to_broadcast(shape),
                        op=ADD,
                    )

            def subtract_on_vector(chunk, difference):
                n, first = chunk[0], chunk[1] + PE_FRAMES * chunk[3] + chunk[4]
                shape = [P, chunk[5], T, PACK]
                nc.vector.tensor_tensor(
                    out=difference[:, chunk[4] :, :, :],
                    in0=qk[:, :, n, 0, first : first + chunk[5]].rearrange("p j g -> p g j").unsqueeze(2).to_broadcast(shape),
                    in1=k_banks[n // 2][:, :, n % 2, :].rearrange("p j t -> p t j").unsqueeze(1).to_broadcast(shape),
                    op=SUBTRACT,
                )

            def regroup(planes, d_grouped):
                width = planes.shape[2] * T
                nc.vector.tensor_copy(
                    out=d_grouped[:, d_grouped.shape[1] - width :, :].rearrange("p (u v) j -> p u j v", v=RUN),
                    in_=planes[:].rearrange("p j g t -> p j (g t)").rearrange("p j (u v) -> p u j v", v=RUN),
                )

            def mix(d_mx, chunk):
                accs = []
                for a in range(O_TILES):
                    acc = psum.tile([P, chunk[2] * T], F32, name="acc")
                    one_pass(nc, acc[:], wr_mx, slice(a * P, (a + 1) * P), d_mx)
                    accs.append(acc)
                return accs

            def store(result, chunk):
                n, g_first, g_count = chunk[0], chunk[1], chunk[2]
                columns = slice(g_first * T, (g_first + g_count) * T)
                nc.sync.dma_start(
                    out=out[n].rearrange("(p a) g t -> p a (g t)", a=O_TILES)[:, :, columns], in_=result[:]
                )

            d_groupeds, accs_of, all_planes = [], [], list(early_planes)
            k_rows, q_rows, pe_banks, differences, inner_done, turned_banks = {}, {}, {}, {}, [], {}
            for n in range(HEAD_TURNS):
                park(n)
            for n in range(HEAD_TURNS):
                load_k(n)

            def difference_of(i):
                if i not in differences:
                    differences[i] = work.tile([P, chunks[i][4] + chunks[i][5], T, PACK], F32, name="difference", bufs=5)
                return differences[i]

            loaded = TURNED_FIRST
            for step in range(len(chunks) + EMPTY_LAG):
                while loaded < len(chunks) and (LOAD_NUM * loaded) // LOAD_DEN - LOAD_BASE <= step:
                    if plain_planes(loaded, 0) < PACK:
                        q_rows[loaded] = load_rows(chunks[loaded])
                    loaded += 1
                if step < len(chunks):
                    chunk = chunks[step]
                    d_groupeds.append(work.tile([P, chunk[2] * T, PACK], BF16, name="d_grouped", align_bytes=64))
                    if step >= EARLY_CHUNKS and planar_frames(chunk) > 0:
                        all_planes.append(new_planes(chunk))
                        for j in range(PACK):
                            tanh_plane(all_planes[step], chunk, j)
                    elif step >= EARLY_CHUNKS:
                        all_planes.append(None)
                    for b, bank in enumerate(pe_banks.get(step, [])):
                        columns = d_groupeds[step][:, 0 : chunk[3] * PE_FRAMES * T, :]
                        nc.scalar.activation(
                            out=columns.rearrange("p (g b t) j -> p b g t j", b=chunk[3], t=T)[:, b],
                            in_=bank[:].rearrange("p j (g t) -> p g t j", t=T),
                            func=TANH,
                        )
                    if step in differences:
                        first = PE_FRAMES * chunk[3] * T
                        nc.scalar.activation(
                            out=d_groupeds[step][:, first : first + (chunk[4] + chunk[5]) * T, :].rearrange("p w j -> p (w j)"),
                            in_=differences[step][:].rearrange("p g t j -> p (g t j)"),
                            func=TANH,
                        )
                if step + 1 < len(chunks) and chunks[step + 1][3] > 0:
                    pe_banks[step + 1] = subtract_on_tensor(step + 1)
                i = step - REGROUP_LAG
                if 0 <= i < len(chunks) and all_planes[i] is not None:
                    regroup(all_planes[i], d_groupeds[i])
                i = step + GATE_AHEAD
                if i < len(chunks) and chunks[i][4] > 0:
                    for n in range(chunks[min(i + INNER_AHEAD, len(chunks) - 1)][0] + 1):
                        if n not in inner_done:
                            inner_done.append(n)
                            side_by_side(n)
                    subtract_on_pool(chunks[i], difference_of(i))
                i = step - QUANT_LAG
                if 0 <= i < len(chunks):
                    d_mx = quantise(nc, work, d_groupeds[i][:].rearrange("p w j -> p (w j)"), "d")
                    accs_of.append(mix(d_mx, chunks[i]))
                i = step + SUB_AHEAD
                if i < len(chunks) and chunks[i][5] > 0:
                    subtract_on_vector(chunks[i], difference_of(i))
                if step in TURN_STEPS:
                    turn_sample(TURN_STEPS.index(step) + HEAD_TURNS)
                if step - TURN_LAG in TURN_STEPS:
                    keep_turned(TURN_STEPS.index(step - TURN_LAG) + HEAD_TURNS)
                    park(TURN_STEPS.index(step - TURN_LAG) + HEAD_TURNS)
                if step - TURN_LAG - K_LAG in TURN_STEPS:
                    load_k(TURN_STEPS.index(step - TURN_LAG - K_LAG) + HEAD_TURNS)
                i = step - EMPTY_LAG
                if 0 <= i < len(chunks):
                    left = len(chunks) - i
                    result = work.tile([P, O_TILES, chunks[i][2] * T], F32, name="result", bufs=RESULT_BUFS)
                    add_second = add_on_scalar if left <= SCALAR_ONE else add_on_vector
                    add_second(nc, result[:, 1, :], accs_of[i][1][:], br_wide[:, 1:2])
                    add_on_vector(nc, result[:, 0, :], accs_of[i][0][:], br_wide[:, 0:1])
                    store(result, chunks[i])
